import numpy as np
import ml_dtypes


def mxq(x, axis, fmt="e4m3"):
    dtype, down = {"e4m3": (ml_dtypes.float8_e4m3fn, 7), "e5m2": (ml_dtypes.float8_e5m2, 14)}[fmt]
    v = np.moveaxis(np.asarray(x, np.float32).astype(ml_dtypes.bfloat16).astype(np.float64), axis, -1)
    blocks = v.reshape(v.shape[:-1] + (-1, 32))
    amax = np.abs(blocks).max(-1, keepdims=True)
    byte = np.maximum(np.where(amax > 0, np.frexp(amax)[1] - 1 + 127, 0) - down, 1)
    scale = np.exp2(byte - 127.0)
    codes = (blocks / scale).astype(np.float32).astype(dtype).astype(np.float64)
    return np.moveaxis((codes * scale).reshape(v.shape), -1, axis)


WIDE = False


def mx_kscale(k):
    if not WIDE:
        return np.ones(k)
    levels = np.array([10, -10, 5, -5, 0])
    a = np.random.permutation(np.resize(levels, k // 512 * 4)).reshape(k // 512, 4)
    idx = np.arange(k)
    return np.exp2(a[idx // 512, idx % 128 // 32])


BF16 = ml_dtypes.bfloat16


def bf(x):
    return np.asarray(x, np.float32).astype(BF16)


def f64(x):
    return np.asarray(x).astype(np.float64)


B, IN_DIM, LAT, OUT_DIM = 8192, 256, 256, 512
G = IN_DIM + LAT


def retanh(v):
    return np.maximum(np.tanh(v), 0.0)


def setup_inputs():
    s = mx_kscale(G)[:IN_DIM]
    d = np.concatenate([s, np.ones(LAT)])[:, None]
    return {
        "x_t": bf(np.random.standard_normal((B, IN_DIM)) * s),
        "h_tminus1": bf(np.random.standard_normal((B, LAT))),
        "gate_noise": bf(np.random.standard_normal((B, LAT)) * 0.3),
        "Wg": bf(np.random.standard_normal((G, LAT)) * 0.8 / np.sqrt(G) / d),
        "bg": bf(np.random.standard_normal(LAT) * 0.2),
        "Wr": bf(np.random.standard_normal((G, LAT)) * 0.8 / np.sqrt(G) / d),
        "br": bf(np.random.standard_normal(LAT) * 0.2),
    }


def reference(x_t, h_tminus1, gate_noise, Wg, bg, Wr, br):
    h_prev = f64(h_tminus1)
    gq = mxq(np.concatenate([f64(x_t), h_prev], axis=1), 1, "e4m3")
    i_t = (gq @ mxq(f64(Wg), 0, "e4m3")) + f64(bg)
    lam = retanh(i_t - f64(gate_noise))
    h_hat = np.tanh((gq @ mxq(f64(Wr), 0, "e4m3")) + f64(br))
    h_t = lam * h_hat + (1.0 - lam) * h_prev
    return h_t, lam

@@ -1,0 +1,263 @@
+from contextlib import ExitStack
+
+import concourse.mybir as mybir
+from concourse.masks import make_identity
+
+FLOPS = 2 * 8192 * 512 * 512
+
+F32 = mybir.dt.float32
+BF16 = mybir.dt.bfloat16
+U32 = mybir.dt.uint32
+U8 = mybir.dt.uint8
+FP8X4 = mybir.dt.float8_e4m3fn_x4
+ALU = mybir.AluOpType
+ACT = mybir.ActivationFunctionType
+
+P = 128
+D = 256
+NT = 64
+QT = 4
+NQ = NT // QT
+LOOKAHEAD = 3
+MANUAL = False
+
+
+def tile_gatel0rdcell_pa_t_kernel(tc, x_t, h_tminus1, gate_noise, Wg, bg, Wr, br, out_0, out_1):
+    nc = tc.nc
+    xv = x_t.rearrange("(p t) k -> p t k", t=NT)
+    hv = h_tminus1.rearrange("(p t) k -> p t k", t=NT)
+    nv = gate_noise.rearrange("(p t) k -> p t k", t=NT)
+    o0v = out_0.rearrange("(p t) k -> p t k", t=NT)
+    o1v = out_1.rearrange("(p t) k -> p t k", t=NT)
+
+    with ExitStack() as ctx:
+        const = ctx.enter_context(tc.tile_pool(name="const", bufs=1))
+        gpool = ctx.enter_context(tc.tile_pool(name="gpool", bufs=LOOKAHEAD + 3))
+        npool = ctx.enter_context(tc.tile_pool(name="npool", bufs=LOOKAHEAD + 1))
+        nbpool = ctx.enter_context(tc.tile_pool(name="nbpool", bufs=4))
+        grpool = ctx.enter_context(tc.tile_pool(name="grpool", bufs=4))
+        cpool = ctx.enter_context(tc.tile_pool(name="cpool", bufs=3))
+        hpool = ctx.enter_context(tc.tile_pool(name="hpool", bufs=6))
+        upool = ctx.enter_context(tc.tile_pool(name="upool", bufs=2))
+        tpool = ctx.enter_context(tc.tile_pool(name="tpool", bufs=3))
+        dpool = ctx.enter_context(tc.tile_pool(name="dpool", bufs=2))
+        opool = ctx.enter_context(tc.tile_pool(name="opool", bufs=3))
+        psum = ctx.enter_context(tc.psum_pool(name="psum", bufs=2))
+
+        g_of = {}
+        nz_of = {}
+        nb_of = {}
+        gc_of = {}
+        gs_of = {}
+        pi_of = {}
+        hT_of = {}
+        t_of = {}
+        d_of = {}
+
+        def load(q):
+            rows = slice(q * QT, (q + 1) * QT)
+            g = gpool.tile([P, QT, 2 * D], BF16)
+            nc.sync.dma_start(out=g[:, :, 0:D], in_=xv[:, rows, :])
+            nc.sync.dma_start(out=g[:, :, D : 2 * D], in_=hv[:, rows, :])
+            nz = npool.tile([P, QT, D], BF16)
+            nc.sync.dma_start(out=nz[:], in_=nv[:, rows, :])
+            g_of[q] = g
+            nz_of[q] = nz
+
+        for q in range(LOOKAHEAD):
+            load(q)
+
+        w_raw = const.tile([P, 2, 4, D], BF16)
+        nc.scalar.dma_start(out=w_raw[:, 0], in_=Wg.rearrange("(p j) w -> p j w", j=4))
+        nc.scalar.dma_start(out=w_raw[:, 1], in_=Wr.rearrange("(p j) w -> p j w", j=4))
+        br_rows = const.tile([P, P], BF16)
+        nc.vector.memset(br_rows[:], 0.0)
+        nc.scalar.dma_start(out=br_rows[0:2, :], in_=br.rearrange("(f p) -> f p", p=P))
+        bg_b = const.tile([P, D], BF16)
+        nc.scalar.dma_start(out=bg_b[:], in_=bg.partition_broadcast(P))
+
+        ident = const.tile([P, P], F32)
+        make_identity(nc, ident[:])
+
+        w_grp = const.tile([P, 2, D, 4], BF16, align_bytes=64)
+        for m in range(2):
+            nc.vector.tensor_copy(out=w_grp[:, m], in_=w_raw[:, m].rearrange("p j w -> p w j"))
+        w_codes = const.tile([P, 2 * D], U32, align_bytes=64)
+        w_scales = const.tile([P, 2 * D], U8, align_bytes=64)
+        nc.vector.quantize_mx(
+            out=w_codes[:].bitcast(FP8X4),
+            scales=w_scales[:],
+            in_=w_grp[:].rearrange("p m w j -> p (m w j)"),
+        )
+
+        br_f32 = const.tile([P, P], F32)
+        nc.vector.tensor_copy(out=br_f32[:], in_=br_rows[:])
+        br_ps = psum.tile([P, 2, D], F32, tag="ph")
+        nc.tensor.transpose(br_ps[:, 0, 0:P], br_f32[:], ident[:])
+        br_col = const.tile([P, 2], F32)
+        nc.vector.tensor_copy(out=br_col[:], in_=br_ps[:, 0, 0:2])
+
+        def noise_bias(q):
+            nb = nbpool.tile([P, QT, D], F32)
+            for i in range(QT):
+                nc.gpsimd.tensor_tensor(out=nb[:, i, :], in0=nz_of[q][:, i, :], in1=bg_b[:], op=ALU.subtract)
+            nb_of[q] = nb
+
+        gt_of = {}
+
+        def g_transposes(q):
+            gw = g_of[q][:].bitcast(F32).rearrange("p t (j e) -> p t e j", e=2)
+            for a in range(2):
+                gt = psum.tile([P, 2, 2, P], F32, tag="gt")
+                for i in range(2):
+                    for e in range(2):
+                        nc.tensor.transpose(gt[:, e, i, :], gw[:, 2 * a + i, e, :], ident[:])
+                gt_of[(q, a)] = gt
+
+        gr_of = {}
+
+        def g_evacuate(q):
+            for a in range(2):
+                gr = grpool.tile([P, 4 * 2 * P], BF16, align_bytes=64)
+                nc.scalar.copy(
+                    out=gr[:].bitcast(F32).rearrange("p (c e) -> p c e", e=2),
+                    in_=gt_of[(q, a)][:].rearrange("p e i l -> p (i l) e"),
+                )
+                gr_of[(q, a)] = gr
+
+        def g_quantise(q):
+            gc = cpool.tile([P, QT * P], U32, align_bytes=64)
+            gs = cpool.tile([P, QT * P], U8, align_bytes=64)
+            for a in range(2):
+                cols = slice(a * 2 * P, (a + 1) * 2 * P)
+                nc.vector.quantize_mx(out=gc[:, cols].bitcast(FP8X4), scales=gs[:, cols], in_=gr_of[(q, a)][:])
+            gc_of[q] = gc
+            gs_of[q] = gs
+
+        pr_of = {}
+
+        def mx(q):
+            gc = gc_of[q]
+            gs = gs_of[q]
+            for f in range(2):
+                pr = psum.tile([P, QT * P], F32, tag="pr")
+                wcols = slice(D + f * P, D + (f + 1) * P)
+                nc.tensor.matmul_mx(
+                    out=pr[:],
+                    lhsT=w_codes[:, wcols].bitcast(FP8X4),
+                    lhsT_scale=w_scales[:, wcols],
+                    rhs=gc[:].bitcast(FP8X4),
+                    rhs_scale=gs[:],
+                    start=True,
+                    stop=True,
+                )
+                pr_of[(q, f)] = pr
+            for a in range(2):
+                pi = psum.tile([P, 2, D], F32, tag="pi")
+                for i in range(2):
+                    cols = slice((2 * a + i) * P, (2 * a + i + 1) * P)
+                    nc.tensor.matmul_mx(
+                        out=pi[:, i, :],
+                        lhsT=gc[:, cols].bitcast(FP8X4),
+                        lhsT_scale=gs[:, cols],
+                        rhs=w_codes[:, 0:D].bitcast(FP8X4),
+                        rhs_scale=w_scales[:, 0:D],
+                        start=True,
+                        stop=True,
+                    )
+                pi_of[(q, a)] = pi
+
+        def tanh_r(q):
+            for f in range(2):
+                hT = hpool.tile([P, QT * P], F32)
+                nc.scalar.activation(out=hT[:], in_=pr_of[(q, f)][:], func=ACT.Tanh, bias=br_col[:, f : f + 1], scale=1.0)
+                hT_of[(q, f)] = hT
+
+        ph_of = {}
+
+        def back_transposes(q):
+            for a in range(2):
+                ph = psum.tile([P, 2, D], F32, tag="ph")
+                for i in range(2):
+                    for f in range(2):
+                        nc.tensor.transpose(
+                            ph[:, i, f * P : (f + 1) * P],
+                            hT_of[(q, f)][:, (2 * a + i) * P : (2 * a + i + 1) * P],
+                            ident[:],
+                        )
+                ph_of[(q, a)] = ph
+
+        u_of = {}
+
+        def gate_arg(q):
+            u = upool.tile([P, QT, D], F32)
+            for a in range(2):
+                nc.vector.tensor_tensor(
+                    out=u[:, 2 * a : 2 * a + 2, :], in0=pi_of[(q, a)][:], in1=nb_of[q][:, 2 * a : 2 * a + 2, :], op=ALU.subtract
+                )
+            u_of[q] = u
+
+        def diff(q):
+            d = dpool.tile([P, QT, D], F32)
+            for a in range(2):
+                nc.vector.tensor_tensor(
+                    out=d[:, 2 * a : 2 * a + 2, :],
+                    in0=ph_of[(q, a)][:],
+                    in1=g_of[q][:, 2 * a : 2 * a + 2, D : 2 * D],
+                    op=ALU.subtract,
+                )
+            d_of[q] = d
+
+        def tanh_i(q):
+            t = tpool.tile([P, QT, D], F32)
+            nc.scalar.activation(out=t[:], in_=u_of[q][:], func=ACT.Tanh)
+            t_of[q] = t
+
+        def gate_out(q):
+            lam = opool.tile([P, QT, D], F32)
+            nc.scalar.activation(out=lam[:], in_=t_of[q][:], func=ACT.Relu)
+            nc.sync.dma_start(out=o1v[:, q * QT : (q + 1) * QT, :], in_=lam[:])
+
+        def mix(q):
+            d = d_of[q]
+            nc.vector.scalar_tensor_tensor(out=d[:], in0=t_of[q][:], scalar=0.0, in1=d[:], op0=ALU.max, op1=ALU.mult)
+            ht = opool.tile([P, QT, D], F32)
+            nc.vector.tensor_tensor(out=ht[:], in0=d[:], in1=g_of[q][:, :, D : 2 * D], op=ALU.add)
+            nc.sync.dma_start(out=o0v[:, q * QT : (q + 1) * QT, :], in_=ht[:])
+
+        def body():
+            noise_bias(0)
+            noise_bias(1)
+            for it in range(-1, NQ + 1):
+                if it >= 0 and it + LOOKAHEAD < NQ:
+                    load(it + LOOKAHEAD)
+                if it >= 0 and it + 2 < NQ:
+                    noise_bias(it + 2)
+                if 0 <= it < NQ:
+                    mx(it)
+                if 0 <= it - 1 < NQ:
+                    back_transposes(it - 1)
+                if it + 1 < NQ:
+                    g_transposes(it + 1)
+                if 0 <= it < NQ:
+                    tanh_r(it)
+                if it + 1 < NQ:
+                    g_evacuate(it + 1)
+                if 0 <= it < NQ:
+                    gate_arg(it)
+                if 0 <= it - 1 < NQ:
+                    diff(it - 1)
+                if it + 1 < NQ:
+                    g_quantise(it + 1)
+                if 0 <= it < NQ:
+                    tanh_i(it)
+                if 0 <= it - 1 < NQ:
+                    mix(it - 1)
+                if 0 <= it < NQ:
+                    gate_out(it)
+
+        if MANUAL:
+            with tc.manual_schedule():
+                body()
+        else:
+            body()

@@ -19,7 +19,7 @@ NT = 64
 QT = 4
 NQ = NT // QT
 LOOKAHEAD = 3
-MANUAL = False
+MANUAL = True
 
 
 def tile_gatel0rdcell_pa_t_kernel(tc, x_t, h_tminus1, gate_noise, Wg, bg, Wr, br, out_0, out_1):

@@ -19,7 +19,8 @@ NT = 64
 QT = 4
 NQ = NT // QT
 LOOKAHEAD = 3
-MANUAL = True
+MANUAL = False
+PE_SUB = 3
 
 
 def tile_gatel0rdcell_pa_t_kernel(tc, x_t, h_tminus1, gate_noise, Wg, bg, Wr, br, out_0, out_1):
@@ -78,6 +79,8 @@ def tile_gatel0rdcell_pa_t_kernel(tc, x_t, h_tminus1, gate_noise, Wg, bg, Wr, br
 
         ident = const.tile([P, P], F32)
         make_identity(nc, ident[:])
+        neg_ident = const.tile([P, P], BF16)
+        nc.vector.tensor_scalar_mul(out=neg_ident[:], in0=ident[:], scalar1=-1.0)
 
         w_grp = const.tile([P, 2, D, 4], BF16, align_bytes=64)
         for m in range(2):
@@ -99,8 +102,9 @@ def tile_gatel0rdcell_pa_t_kernel(tc, x_t, h_tminus1, gate_noise, Wg, bg, Wr, br
 
         def noise_bias(q):
             nb = nbpool.tile([P, QT, D], F32)
-            for i in range(QT):
-                nc.gpsimd.tensor_tensor(out=nb[:, i, :], in0=nz_of[q][:, i, :], in1=bg_b[:], op=ALU.subtract)
+            nc.vector.tensor_tensor(
+                out=nb[:], in0=nz_of[q][:], in1=bg_b[:].unsqueeze(1).to_broadcast([P, QT, D]), op=ALU.subtract
+            )
             nb_of[q] = nb
 
         gt_of = {}
@@ -179,11 +183,19 @@ def tile_gatel0rdcell_pa_t_kernel(tc, x_t, h_tminus1, gate_noise, Wg, bg, Wr, br
             for a in range(2):
                 ph = psum.tile([P, 2, D], F32, tag="ph")
                 for i in range(2):
+                    sub = 2 * a + i < PE_SUB
+                    if sub:
+                        nc.tensor.matmul(
+                            out=ph[:, i, :], lhsT=neg_ident[:], rhs=g_of[q][:, 2 * a + i, D : 2 * D], start=True, stop=False
+                        )
                     for f in range(2):
-                        nc.tensor.transpose(
-                            ph[:, i, f * P : (f + 1) * P],
-                            hT_of[(q, f)][:, (2 * a + i) * P : (2 * a + i + 1) * P],
-                            ident[:],
+                        nc.tensor.matmul(
+                            out=ph[:, i, f * P : (f + 1) * P],
+                            lhsT=hT_of[(q, f)][:, (2 * a + i) * P : (2 * a + i + 1) * P],
+                            rhs=ident[:],
+                            is_transpose=True,
+                            start=not sub,
+                            stop=(f == 1) or not sub,
                         )
                 ph_of[(q, a)] = ph
 
@@ -199,13 +211,11 @@ def tile_gatel0rdcell_pa_t_kernel(tc, x_t, h_tminus1, gate_noise, Wg, bg, Wr, br
 
         def diff(q):
             d = dpool.tile([P, QT, D], F32)
-            for a in range(2):
-                nc.vector.tensor_tensor(
-                    out=d[:, 2 * a : 2 * a + 2, :],
-                    in0=ph_of[(q, a)][:],
-                    in1=g_of[q][:, 2 * a : 2 * a + 2, D : 2 * D],
-                    op=ALU.subtract,
-                )
+            t = t_of[q]
+            nc.vector.scalar_tensor_tensor(out=d[:, 0:2, :], in0=t[:, 0:2, :], scalar=0.0, in1=ph_of[(q, 0)][:], op0=ALU.max, op1=ALU.mult)
+            nc.vector.scalar_tensor_tensor(out=d[:, 2, :], in0=t[:, 2, :], scalar=0.0, in1=ph_of[(q, 1)][:, 0, :], op0=ALU.max, op1=ALU.mult)
+            nc.vector.tensor_tensor(out=d[:, 3, :], in0=ph_of[(q, 1)][:, 1, :], in1=g_of[q][:, 3, D : 2 * D], op=ALU.subtract)
+            nc.vector.scalar_tensor_tensor(out=d[:, 3, :], in0=t[:, 3, :], scalar=0.0, in1=d[:, 3, :], op0=ALU.max, op1=ALU.mult)
             d_of[q] = d
 
         def tanh_i(q):
@@ -220,7 +230,6 @@ def tile_gatel0rdcell_pa_t_kernel(tc, x_t, h_tminus1, gate_noise, Wg, bg, Wr, br
 
         def mix(q):
             d = d_of[q]
-            nc.vector.scalar_tensor_tensor(out=d[:], in0=t_of[q][:], scalar=0.0, in1=d[:], op0=ALU.max, op1=ALU.mult)
             ht = opool.tile([P, QT, D], F32)
             nc.vector.tensor_tensor(out=ht[:], in0=d[:], in1=g_of[q][:, :, D : 2 * D], op=ALU.add)
             nc.sync.dma_start(out=o0v[:, q * QT : (q + 1) * QT, :], in_=ht[:])
@@ -231,8 +240,6 @@ def tile_gatel0rdcell_pa_t_kernel(tc, x_t, h_tminus1, gate_noise, Wg, bg, Wr, br
             for it in range(-1, NQ + 1):
                 if it >= 0 and it + LOOKAHEAD < NQ:
                     load(it + LOOKAHEAD)
-                if it >= 0 and it + 2 < NQ:
-                    noise_bias(it + 2)
                 if 0 <= it < NQ:
                     mx(it)
                 if 0 <= it - 1 < NQ:
@@ -253,6 +260,8 @@ def tile_gatel0rdcell_pa_t_kernel(tc, x_t, h_tminus1, gate_noise, Wg, bg, Wr, br
                     tanh_i(it)
                 if 0 <= it - 1 < NQ:
                     mix(it - 1)
+                if it >= 0 and it + 2 < NQ:
+                    noise_bias(it + 2)
                 if 0 <= it < NQ:
                     gate_out(it)
 

@@ -16,15 +16,21 @@ ACT = mybir.ActivationFunctionType
 P = 128
 D = 256
 NT = 64
-QT = 4
-NQ = NT // QT
-LOOKAHEAD = 3
+UNITS = (2, 2, 4, 4, 4, 4, 4, 4, 4, 4, 4, 4, 4, 4, 4, 4, 2, 2)
+NU = 18
+LOOKAHEAD = 4
 MANUAL = False
-PE_SUB = 3
+LAM_ON_VECTOR = True
+
+
+def noise_on_tensor_engine(q):
+    return q not in (4, 7, 10, 13)
 
 
 def tile_gatel0rdcell_pa_t_kernel(tc, x_t, h_tminus1, gate_noise, Wg, bg, Wr, br, out_0, out_1):
     nc = tc.nc
+    assert len(UNITS) == NU and sum(UNITS) == NT
+    FIRST = [sum(UNITS[:u]) for u in range(NU)]
     xv = x_t.rearrange("(p t) k -> p t k", t=NT)
     hv = h_tminus1.rearrange("(p t) k -> p t k", t=NT)
     nv = gate_noise.rearrange("(p t) k -> p t k", t=NT)
@@ -33,49 +39,62 @@ def tile_gatel0rdcell_pa_t_kernel(tc, x_t, h_tminus1, gate_noise, Wg, bg, Wr, br
 
     with ExitStack() as ctx:
         const = ctx.enter_context(tc.tile_pool(name="const", bufs=1))
-        gpool = ctx.enter_context(tc.tile_pool(name="gpool", bufs=LOOKAHEAD + 3))
-        npool = ctx.enter_context(tc.tile_pool(name="npool", bufs=LOOKAHEAD + 1))
-        nbpool = ctx.enter_context(tc.tile_pool(name="nbpool", bufs=4))
+        gpool = ctx.enter_context(tc.tile_pool(name="gpool", bufs=LOOKAHEAD + 4))
+        npool = ctx.enter_context(tc.tile_pool(name="npool", bufs=LOOKAHEAD + 3))
         grpool = ctx.enter_context(tc.tile_pool(name="grpool", bufs=4))
         cpool = ctx.enter_context(tc.tile_pool(name="cpool", bufs=3))
-        hpool = ctx.enter_context(tc.tile_pool(name="hpool", bufs=6))
+        hpool = ctx.enter_context(tc.tile_pool(name="hpool", bufs=4))
+        ipool = ctx.enter_context(tc.tile_pool(name="ipool", bufs=6))
         upool = ctx.enter_context(tc.tile_pool(name="upool", bufs=2))
         tpool = ctx.enter_context(tc.tile_pool(name="tpool", bufs=3))
-        dpool = ctx.enter_context(tc.tile_pool(name="dpool", bufs=2))
+        dpool = ctx.enter_context(tc.tile_pool(name="dpool", bufs=3))
         opool = ctx.enter_context(tc.tile_pool(name="opool", bufs=3))
         psum = ctx.enter_context(tc.psum_pool(name="psum", bufs=2))
 
         g_of = {}
         nz_of = {}
-        nb_of = {}
+        gt_of = {}
+        gr_of = {}
         gc_of = {}
         gs_of = {}
-        pi_of = {}
+        pt_of = {}
         hT_of = {}
+        iT_of = {}
+        ph_of = {}
+        pu_of = {}
         t_of = {}
         d_of = {}
 
-        def load(q):
-            rows = slice(q * QT, (q + 1) * QT)
-            g = gpool.tile([P, QT, 2 * D], BF16)
-            nc.sync.dma_start(out=g[:, :, 0:D], in_=xv[:, rows, :])
-            nc.sync.dma_start(out=g[:, :, D : 2 * D], in_=hv[:, rows, :])
-            nz = npool.tile([P, QT, D], BF16)
-            nc.sync.dma_start(out=nz[:], in_=nv[:, rows, :])
+        def rows_of(q):
+            return slice(FIRST[q], FIRST[q] + UNITS[q])
+
+        def load_g(q):
+            g = gpool.tile([P, UNITS[q], 2 * D], BF16)
+            nc.sync.dma_start(out=g[:, :, 0:D], in_=xv[:, rows_of(q), :])
+            nc.sync.dma_start(out=g[:, :, D : 2 * D], in_=hv[:, rows_of(q), :])
             g_of[q] = g
+
+        def load_n(q):
+            nz = npool.tile([P, UNITS[q], D], BF16)
+            nc.sync.dma_start(out=nz[:], in_=nv[:, rows_of(q), :])
             nz_of[q] = nz
 
-        for q in range(LOOKAHEAD):
-            load(q)
+        load_g(0)
+        for q in range(1, LOOKAHEAD):
+            load_g(q)
+            load_n(q - 1)
 
+        warm = const.tile([P, 1], F32)
+        nc.vector.memset(warm[:], 0.0)
+        nc.scalar.activation(out=warm[:], in_=warm[:], func=ACT.Tanh)
+
+        b_rows = const.tile([P, P], BF16)
+        nc.vector.memset(b_rows[:], 0.0)
+        nc.scalar.dma_start(out=b_rows[0:2, :], in_=bg.rearrange("(f p) -> f p", p=P))
+        nc.scalar.dma_start(out=b_rows[2:4, :], in_=br.rearrange("(f p) -> f p", p=P))
         w_raw = const.tile([P, 2, 4, D], BF16)
         nc.scalar.dma_start(out=w_raw[:, 0], in_=Wg.rearrange("(p j) w -> p j w", j=4))
         nc.scalar.dma_start(out=w_raw[:, 1], in_=Wr.rearrange("(p j) w -> p j w", j=4))
-        br_rows = const.tile([P, P], BF16)
-        nc.vector.memset(br_rows[:], 0.0)
-        nc.scalar.dma_start(out=br_rows[0:2, :], in_=br.rearrange("(f p) -> f p", p=P))
-        bg_b = const.tile([P, D], BF16)
-        nc.scalar.dma_start(out=bg_b[:], in_=bg.partition_broadcast(P))
 
         ident = const.tile([P, P], F32)
         make_identity(nc, ident[:])
@@ -93,35 +112,24 @@ def tile_gatel0rdcell_pa_t_kernel(tc, x_t, h_tminus1, gate_noise, Wg, bg, Wr, br
             in_=w_grp[:].rearrange("p m w j -> p (m w j)"),
         )
 
-        br_f32 = const.tile([P, P], F32)
-        nc.vector.tensor_copy(out=br_f32[:], in_=br_rows[:])
-        br_ps = psum.tile([P, 2, D], F32, tag="ph")
-        nc.tensor.transpose(br_ps[:, 0, 0:P], br_f32[:], ident[:])
-        br_col = const.tile([P, 2], F32)
-        nc.vector.tensor_copy(out=br_col[:], in_=br_ps[:, 0, 0:2])
-
-        def noise_bias(q):
-            nb = nbpool.tile([P, QT, D], F32)
-            nc.vector.tensor_tensor(
-                out=nb[:], in0=nz_of[q][:], in1=bg_b[:].unsqueeze(1).to_broadcast([P, QT, D]), op=ALU.subtract
-            )
-            nb_of[q] = nb
-
-        gt_of = {}
+        b_f32 = const.tile([P, P], F32)
+        nc.vector.tensor_copy(out=b_f32[:], in_=b_rows[:])
+        b_ps = psum.tile([P, 2, D], F32, tag="ph")
+        nc.tensor.transpose(b_ps[:, 0, 0:P], b_f32[:], ident[:])
+        b_col = const.tile([P, 4], F32)
+        nc.vector.tensor_copy(out=b_col[:], in_=b_ps[:, 0, 0:4])
 
         def g_transposes(q):
             gw = g_of[q][:].bitcast(F32).rearrange("p t (j e) -> p t e j", e=2)
-            for a in range(2):
+            for a in range(UNITS[q] // 2):
                 gt = psum.tile([P, 2, 2, P], F32, tag="gt")
                 for i in range(2):
                     for e in range(2):
                         nc.tensor.transpose(gt[:, e, i, :], gw[:, 2 * a + i, e, :], ident[:])
                 gt_of[(q, a)] = gt
 
-        gr_of = {}
-
         def g_evacuate(q):
-            for a in range(2):
+            for a in range(UNITS[q] // 2):
                 gr = grpool.tile([P, 4 * 2 * P], BF16, align_bytes=64)
                 nc.scalar.copy(
                     out=gr[:].bitcast(F32).rearrange("p (c e) -> p c e", e=2),
@@ -130,140 +138,151 @@ def tile_gatel0rdcell_pa_t_kernel(tc, x_t, h_tminus1, gate_noise, Wg, bg, Wr, br
                 gr_of[(q, a)] = gr
 
         def g_quantise(q):
-            gc = cpool.tile([P, QT * P], U32, align_bytes=64)
-            gs = cpool.tile([P, QT * P], U8, align_bytes=64)
-            for a in range(2):
+            gc = cpool.tile([P, UNITS[q] * P], U32, align_bytes=64)
+            gs = cpool.tile([P, UNITS[q] * P], U8, align_bytes=64)
+            for a in range(UNITS[q] // 2):
                 cols = slice(a * 2 * P, (a + 1) * 2 * P)
                 nc.vector.quantize_mx(out=gc[:, cols].bitcast(FP8X4), scales=gs[:, cols], in_=gr_of[(q, a)][:])
             gc_of[q] = gc
             gs_of[q] = gs
 
-        pr_of = {}
-
-        def mx(q):
-            gc = gc_of[q]
-            gs = gs_of[q]
-            for f in range(2):
-                pr = psum.tile([P, QT * P], F32, tag="pr")
-                wcols = slice(D + f * P, D + (f + 1) * P)
+        def mx(q, first):
+            for w in range(first, first + 2):
+                pt = psum.tile([P, UNITS[q] * P], F32, tag="pt")
+                wcols = slice(w * P, (w + 1) * P)
                 nc.tensor.matmul_mx(
-                    out=pr[:],
+                    out=pt[:],
                     lhsT=w_codes[:, wcols].bitcast(FP8X4),
                     lhsT_scale=w_scales[:, wcols],
-                    rhs=gc[:].bitcast(FP8X4),
-                    rhs_scale=gs[:],
+                    rhs=gc_of[q][:].bitcast(FP8X4),
+                    rhs_scale=gs_of[q][:],
                     start=True,
                     stop=True,
                 )
-                pr_of[(q, f)] = pr
-            for a in range(2):
-                pi = psum.tile([P, 2, D], F32, tag="pi")
-                for i in range(2):
-                    cols = slice((2 * a + i) * P, (2 * a + i + 1) * P)
-                    nc.tensor.matmul_mx(
-                        out=pi[:, i, :],
-                        lhsT=gc[:, cols].bitcast(FP8X4),
-                        lhsT_scale=gs[:, cols],
-                        rhs=w_codes[:, 0:D].bitcast(FP8X4),
-                        rhs_scale=w_scales[:, 0:D],
-                        start=True,
-                        stop=True,
-                    )
-                pi_of[(q, a)] = pi
+                pt_of[(q, w)] = pt
 
         def tanh_r(q):
             for f in range(2):
-                hT = hpool.tile([P, QT * P], F32)
-                nc.scalar.activation(out=hT[:], in_=pr_of[(q, f)][:], func=ACT.Tanh, bias=br_col[:, f : f + 1], scale=1.0)
+                hT = hpool.tile([P, UNITS[q] * P], F32)
+                nc.scalar.activation(
+                    out=hT[:], in_=pt_of[(q, 2 + f)][:], func=ACT.Tanh, bias=b_col[:, 2 + f : 3 + f], scale=1.0
+                )
                 hT_of[(q, f)] = hT
 
-        ph_of = {}
+        def bias_i(q):
+            for f in range(2):
+                iT = ipool.tile([P, UNITS[q] * P], F32)
+                nc.scalar.activation(
+                    out=iT[:], in_=pt_of[(q, f)][:], func=ACT.Identity, bias=b_col[:, f : f + 1], scale=1.0
+                )
+                iT_of[(q, f)] = iT
 
-        def back_transposes(q):
-            for a in range(2):
+        def back_r(q):
+            for a in range(UNITS[q] // 2):
                 ph = psum.tile([P, 2, D], F32, tag="ph")
                 for i in range(2):
-                    sub = 2 * a + i < PE_SUB
+                    for f in range(2):
+                        nc.tensor.transpose(
+                            ph[:, i, f * P : (f + 1) * P],
+                            hT_of[(q, f)][:, (2 * a + i) * P : (2 * a + i + 1) * P],
+                            ident[:],
+                        )
+                ph_of[(q, a)] = ph
+
+        def back_i(q):
+            sub = noise_on_tensor_engine(q)
+            for a in range(UNITS[q] // 2):
+                pu = psum.tile([P, 2, D], F32, tag="pu")
+                for i in range(2):
                     if sub:
                         nc.tensor.matmul(
-                            out=ph[:, i, :], lhsT=neg_ident[:], rhs=g_of[q][:, 2 * a + i, D : 2 * D], start=True, stop=False
+                            out=pu[:, i, :], lhsT=neg_ident[:], rhs=nz_of[q][:, 2 * a + i, :], start=True, stop=False
                         )
                     for f in range(2):
                         nc.tensor.matmul(
-                            out=ph[:, i, f * P : (f + 1) * P],
-                            lhsT=hT_of[(q, f)][:, (2 * a + i) * P : (2 * a + i + 1) * P],
+                            out=pu[:, i, f * P : (f + 1) * P],
+                            lhsT=iT_of[(q, f)][:, (2 * a + i) * P : (2 * a + i + 1) * P],
                             rhs=ident[:],
                             is_transpose=True,
                             start=not sub,
                             stop=(f == 1) or not sub,
                         )
-                ph_of[(q, a)] = ph
-
-        u_of = {}
-
-        def gate_arg(q):
-            u = upool.tile([P, QT, D], F32)
-            for a in range(2):
-                nc.vector.tensor_tensor(
-                    out=u[:, 2 * a : 2 * a + 2, :], in0=pi_of[(q, a)][:], in1=nb_of[q][:, 2 * a : 2 * a + 2, :], op=ALU.subtract
-                )
-            u_of[q] = u
-
-        def diff(q):
-            d = dpool.tile([P, QT, D], F32)
-            t = t_of[q]
-            nc.vector.scalar_tensor_tensor(out=d[:, 0:2, :], in0=t[:, 0:2, :], scalar=0.0, in1=ph_of[(q, 0)][:], op0=ALU.max, op1=ALU.mult)
-            nc.vector.scalar_tensor_tensor(out=d[:, 2, :], in0=t[:, 2, :], scalar=0.0, in1=ph_of[(q, 1)][:, 0, :], op0=ALU.max, op1=ALU.mult)
-            nc.vector.tensor_tensor(out=d[:, 3, :], in0=ph_of[(q, 1)][:, 1, :], in1=g_of[q][:, 3, D : 2 * D], op=ALU.subtract)
-            nc.vector.scalar_tensor_tensor(out=d[:, 3, :], in0=t[:, 3, :], scalar=0.0, in1=d[:, 3, :], op0=ALU.max, op1=ALU.mult)
-            d_of[q] = d
+                pu_of[(q, a)] = pu
 
         def tanh_i(q):
-            t = tpool.tile([P, QT, D], F32)
-            nc.scalar.activation(out=t[:], in_=u_of[q][:], func=ACT.Tanh)
+            t = tpool.tile([P, UNITS[q], D], F32)
+            if noise_on_tensor_engine(q):
+                for a in range(UNITS[q] // 2):
+                    nc.scalar.activation(out=t[:, 2 * a : 2 * a + 2, :], in_=pu_of[(q, a)][:], func=ACT.Tanh)
+            else:
+                u = upool.tile([P, UNITS[q], D], F32)
+                for a in range(UNITS[q] // 2):
+                    nc.vector.tensor_tensor(
+                        out=u[:, 2 * a : 2 * a + 2, :],
+                        in0=pu_of[(q, a)][:],
+                        in1=nz_of[q][:, 2 * a : 2 * a + 2, :],
+                        op=ALU.subtract,
+                    )
+                nc.scalar.activation(out=t[:], in_=u[:], func=ACT.Tanh)
             t_of[q] = t
 
-        def gate_out(q):
-            lam = opool.tile([P, QT, D], F32)
-            nc.scalar.activation(out=lam[:], in_=t_of[q][:], func=ACT.Relu)
-            nc.sync.dma_start(out=o1v[:, q * QT : (q + 1) * QT, :], in_=lam[:])
+        def diff(q):
+            d = dpool.tile([P, UNITS[q], D], F32)
+            for a in range(UNITS[q] // 2):
+                nc.vector.tensor_tensor(
+                    out=d[:, 2 * a : 2 * a + 2, :],
+                    in0=ph_of[(q, a)][:],
+                    in1=g_of[q][:, 2 * a : 2 * a + 2, D : 2 * D],
+                    op=ALU.subtract,
+                )
+            d_of[q] = d
 
-        def mix(q):
+        def gated(q):
+            lam = opool.tile([P, UNITS[q], D], F32)
+            if LAM_ON_VECTOR:
+                nc.vector.tensor_scalar_max(out=lam[:], in0=t_of[q][:], scalar1=0.0)
+            else:
+                nc.scalar.activation(out=lam[:], in_=t_of[q][:], func=ACT.Relu)
+            nc.sync.dma_start(out=o1v[:, rows_of(q), :], in_=lam[:])
             d = d_of[q]
-            ht = opool.tile([P, QT, D], F32)
-            nc.vector.tensor_tensor(out=ht[:], in0=d[:], in1=g_of[q][:, :, D : 2 * D], op=ALU.add)
-            nc.sync.dma_start(out=o0v[:, q * QT : (q + 1) * QT, :], in_=ht[:])
+            nc.vector.scalar_tensor_tensor(out=d[:], in0=t_of[q][:], scalar=0.0, in1=d[:], op0=ALU.max, op1=ALU.mult)
+
+        def outputs(q):
+            ht = opool.tile([P, UNITS[q], D], F32)
+            nc.vector.tensor_tensor(out=ht[:], in0=d_of[q][:], in1=g_of[q][:, :, D : 2 * D], op=ALU.add)
+            nc.sync.dma_start(out=o0v[:, rows_of(q), :], in_=ht[:])
+
+        def on(q):
+            return 0 <= q < NU
 
         def body():
-            noise_bias(0)
-            noise_bias(1)
-            for it in range(-1, NQ + 1):
-                if it >= 0 and it + LOOKAHEAD < NQ:
-                    load(it + LOOKAHEAD)
-                if 0 <= it < NQ:
-                    mx(it)
-                if 0 <= it - 1 < NQ:
-                    back_transposes(it - 1)
-                if it + 1 < NQ:
-                    g_transposes(it + 1)
-                if 0 <= it < NQ:
+            for it in range(-1, NU + 2):
+                if it >= 0 and on(it + LOOKAHEAD):
+                    load_g(it + LOOKAHEAD)
+                if it >= 0 and on(it + LOOKAHEAD - 1):
+                    load_n(it + LOOKAHEAD - 1)
+                if on(it):
+                    mx(it, 2)
                     tanh_r(it)
-                if it + 1 < NQ:
-                    g_evacuate(it + 1)
-                if 0 <= it < NQ:
-                    gate_arg(it)
-                if 0 <= it - 1 < NQ:
+                if on(it - 2):
+                    tanh_i(it - 2)
+                if on(it - 1):
                     diff(it - 1)
-                if it + 1 < NQ:
+                if on(it + 1):
+                    g_transposes(it + 1)
+                    g_evacuate(it + 1)
+                if on(it):
+                    mx(it, 0)
+                    bias_i(it)
+                    back_r(it)
+                if on(it - 1):
+                    back_i(it - 1)
+                if on(it - 2):
+                    gated(it - 2)
+                if on(it + 1):
                     g_quantise(it + 1)
-                if 0 <= it < NQ:
-                    tanh_i(it)
-                if 0 <= it - 1 < NQ:
-                    mix(it - 1)
-                if it >= 0 and it + 2 < NQ:
-                    noise_bias(it + 2)
-                if 0 <= it < NQ:
-                    gate_out(it)
+                if on(it - 2):
+                    outputs(it - 2)
 
         if MANUAL:
             with tc.manual_schedule():

@@ -19,7 +19,7 @@ NT = 64
 UNITS = (2, 2, 4, 4, 4, 4, 4, 4, 4, 4, 4, 4, 4, 4, 4, 4, 2, 2)
 NU = 18
 LOOKAHEAD = 4
-MANUAL = False
+MANUAL = True
 LAM_ON_VECTOR = True
 
 
@@ -256,7 +256,7 @@ def tile_gatel0rdcell_pa_t_kernel(tc, x_t, h_tminus1, gate_noise, Wg, bg, Wr, br
             return 0 <= q < NU
 
         def body():
-            for it in range(-1, NU + 2):
+            for it in range(-1, NU + 3):
                 if it >= 0 and on(it + LOOKAHEAD):
                     load_g(it + LOOKAHEAD)
                 if it >= 0 and on(it + LOOKAHEAD - 1):
@@ -268,6 +268,8 @@ def tile_gatel0rdcell_pa_t_kernel(tc, x_t, h_tminus1, gate_noise, Wg, bg, Wr, br
                     tanh_i(it - 2)
                 if on(it - 1):
                     diff(it - 1)
+                if on(it - 3):
+                    outputs(it - 3)
                 if on(it + 1):
                     g_transposes(it + 1)
                     g_evacuate(it + 1)
@@ -281,8 +283,6 @@ def tile_gatel0rdcell_pa_t_kernel(tc, x_t, h_tminus1, gate_noise, Wg, bg, Wr, br
                     gated(it - 2)
                 if on(it + 1):
                     g_quantise(it + 1)
-                if on(it - 2):
-                    outputs(it - 2)
 
         if MANUAL:
             with tc.manual_schedule():

@@ -19,7 +19,7 @@ NT = 64
 UNITS = (2, 2, 4, 4, 4, 4, 4, 4, 4, 4, 4, 4, 4, 4, 4, 4, 2, 2)
 NU = 18
 LOOKAHEAD = 4
-MANUAL = True
+MANUAL = False
 LAM_ON_VECTOR = True
 
 
@@ -191,23 +191,25 @@ def tile_gatel0rdcell_pa_t_kernel(tc, x_t, h_tminus1, gate_noise, Wg, bg, Wr, br
 
         def back_i(q):
             sub = noise_on_tensor_engine(q)
-            for a in range(UNITS[q] // 2):
+            pairs = range(UNITS[q] // 2)
+            for a in pairs:
                 pu = psum.tile([P, 2, D], F32, tag="pu")
+                if sub:
+                    nc.tensor.matmul(
+                        out=pu[:], lhsT=neg_ident[:], rhs=nz_of[q][:, 2 * a : 2 * a + 2, :], start=True, stop=False
+                    )
+                pu_of[(q, a)] = pu
+            for a in pairs:
                 for i in range(2):
-                    if sub:
-                        nc.tensor.matmul(
-                            out=pu[:, i, :], lhsT=neg_ident[:], rhs=nz_of[q][:, 2 * a + i, :], start=True, stop=False
-                        )
                     for f in range(2):
                         nc.tensor.matmul(
-                            out=pu[:, i, f * P : (f + 1) * P],
+                            out=pu_of[(q, a)][:, i, f * P : (f + 1) * P],
                             lhsT=iT_of[(q, f)][:, (2 * a + i) * P : (2 * a + i + 1) * P],
                             rhs=ident[:],
                             is_transpose=True,
                             start=not sub,
-                            stop=(f == 1) or not sub,
+                            stop=(i == 1 and f == 1) or not sub,
                         )
-                pu_of[(q, a)] = pu
 
         def tanh_i(q):
             t = tpool.tile([P, UNITS[q], D], F32)
@@ -256,7 +258,7 @@ def tile_gatel0rdcell_pa_t_kernel(tc, x_t, h_tminus1, gate_noise, Wg, bg, Wr, br
             return 0 <= q < NU
 
         def body():
-            for it in range(-1, NU + 3):
+            for it in range(-1, NU + 2):
                 if it >= 0 and on(it + LOOKAHEAD):
                     load_g(it + LOOKAHEAD)
                 if it >= 0 and on(it + LOOKAHEAD - 1):
@@ -268,8 +270,6 @@ def tile_gatel0rdcell_pa_t_kernel(tc, x_t, h_tminus1, gate_noise, Wg, bg, Wr, br
                     tanh_i(it - 2)
                 if on(it - 1):
                     diff(it - 1)
-                if on(it - 3):
-                    outputs(it - 3)
                 if on(it + 1):
                     g_transposes(it + 1)
                     g_evacuate(it + 1)
@@ -283,6 +283,8 @@ def tile_gatel0rdcell_pa_t_kernel(tc, x_t, h_tminus1, gate_noise, Wg, bg, Wr, br
                     gated(it - 2)
                 if on(it + 1):
                     g_quantise(it + 1)
+                if on(it - 2):
+                    outputs(it - 2)
 
         if MANUAL:
             with tc.manual_schedule():

@@ -20,7 +20,6 @@ UNITS = (2, 2, 4, 4, 4, 4, 4, 4, 4, 4, 4, 4, 4, 4, 4, 4, 2, 2)
 NU = 18
 LOOKAHEAD = 4
 MANUAL = False
-LAM_ON_VECTOR = True
 
 
 def noise_on_tensor_engine(q):
@@ -241,10 +240,15 @@ def tile_gatel0rdcell_pa_t_kernel(tc, x_t, h_tminus1, gate_noise, Wg, bg, Wr, br
 
         def gated(q):
             lam = opool.tile([P, UNITS[q], D], F32)
-            if LAM_ON_VECTOR:
-                nc.vector.tensor_scalar_max(out=lam[:], in0=t_of[q][:], scalar1=0.0)
-            else:
-                nc.scalar.activation(out=lam[:], in_=t_of[q][:], func=ACT.Relu)
+            for a in range(UNITS[q] // 2):
+                nc.gpsimd.tensor_scalar(
+                    out=lam[:, 2 * a : 2 * a + 2, :],
+                    in0=t_of[q][:, 2 * a : 2 * a + 2, :],
+                    scalar1=0.0,
+                    scalar2=0.0,
+                    op0=ALU.max,
+                    op1=ALU.add,
+                )
             nc.sync.dma_start(out=o1v[:, rows_of(q), :], in_=lam[:])
             d = d_of[q]
             nc.vector.scalar_tensor_tensor(out=d[:], in0=t_of[q][:], scalar=0.0, in1=d[:], op0=ALU.max, op1=ALU.mult)

@@ -22,8 +22,8 @@ LOOKAHEAD = 4
 MANUAL = False
 
 
-def noise_on_tensor_engine(q):
-    return q not in (4, 7, 10, 13)
+def gate_in_rows(q):
+    return q < 5
 
 
 def tile_gatel0rdcell_pa_t_kernel(tc, x_t, h_tminus1, gate_noise, Wg, bg, Wr, br, out_0, out_1):
@@ -45,6 +45,7 @@ def tile_gatel0rdcell_pa_t_kernel(tc, x_t, h_tminus1, gate_noise, Wg, bg, Wr, br
         hpool = ctx.enter_context(tc.tile_pool(name="hpool", bufs=4))
         ipool = ctx.enter_context(tc.tile_pool(name="ipool", bufs=6))
         upool = ctx.enter_context(tc.tile_pool(name="upool", bufs=2))
+        nbpool = ctx.enter_context(tc.tile_pool(name="nbpool", bufs=5))
         tpool = ctx.enter_context(tc.tile_pool(name="tpool", bufs=3))
         dpool = ctx.enter_context(tc.tile_pool(name="dpool", bufs=3))
         opool = ctx.enter_context(tc.tile_pool(name="opool", bufs=3))
@@ -78,10 +79,28 @@ def tile_gatel0rdcell_pa_t_kernel(tc, x_t, h_tminus1, gate_noise, Wg, bg, Wr, br
             nc.sync.dma_start(out=nz[:], in_=nv[:, rows_of(q), :])
             nz_of[q] = nz
 
+        bg_row = const.tile([P, D], BF16)
+        nc.vector.memset(bg_row[:], 0.0)
+        nc.scalar.dma_start(out=bg_row[0:1, :], in_=bg.rearrange("(o n) -> o n", o=1))
+        ones = const.tile([P, P], BF16)
+        nc.vector.memset(ones[:], 1.0)
+        bg_ps = psum.tile([P, 2, D], F32, tag="pu")
+        nc.tensor.matmul(out=bg_ps[:, 0, :], lhsT=ones[:], rhs=bg_row[:], start=True, stop=True)
+        bg_b = const.tile([P, D], F32)
+        nc.vector.tensor_copy(out=bg_b[:], in_=bg_ps[:, 0, :])
+        nb_of = {}
+
+        def noise_bias(q):
+            nb = nbpool.tile([P, UNITS[q], D], F32)
+            nc.vector.tensor_tensor(
+                out=nb[:], in0=nz_of[q][:], in1=bg_b[:].unsqueeze(1).to_broadcast([P, UNITS[q], D]), op=ALU.subtract
+            )
+            nb_of[q] = nb
+
         load_g(0)
         for q in range(1, LOOKAHEAD):
-            load_g(q)
             load_n(q - 1)
+            load_g(q)
 
         warm = const.tile([P, 1], F32)
         nc.vector.memset(warm[:], 0.0)
@@ -160,6 +179,22 @@ def tile_gatel0rdcell_pa_t_kernel(tc, x_t, h_tminus1, gate_noise, Wg, bg, Wr, br
                 )
                 pt_of[(q, w)] = pt
 
+        def mx_gate_rows(q):
+            for a in range(UNITS[q] // 2):
+                pu = psum.tile([P, 2, D], F32, tag="pu")
+                for i in range(2):
+                    cols = slice((2 * a + i) * P, (2 * a + i + 1) * P)
+                    nc.tensor.matmul_mx(
+                        out=pu[:, i, :],
+                        lhsT=gc_of[q][:, cols].bitcast(FP8X4),
+                        lhsT_scale=gs_of[q][:, cols],
+                        rhs=w_codes[:, 0:D].bitcast(FP8X4),
+                        rhs_scale=w_scales[:, 0:D],
+                        start=True,
+                        stop=True,
+                    )
+                pu_of[(q, a)] = pu
+
         def tanh_r(q):
             for f in range(2):
                 hT = hpool.tile([P, UNITS[q] * P], F32)
@@ -189,7 +224,7 @@ def tile_gatel0rdcell_pa_t_kernel(tc, x_t, h_tminus1, gate_noise, Wg, bg, Wr, br
                 ph_of[(q, a)] = ph
 
         def back_i(q):
-            sub = noise_on_tensor_engine(q)
+            sub = True
             pairs = range(UNITS[q] // 2)
             for a in pairs:
                 pu = psum.tile([P, 2, D], F32, tag="pu")
@@ -212,7 +247,7 @@ def tile_gatel0rdcell_pa_t_kernel(tc, x_t, h_tminus1, gate_noise, Wg, bg, Wr, br
 
         def tanh_i(q):
             t = tpool.tile([P, UNITS[q], D], F32)
-            if noise_on_tensor_engine(q):
+            if not gate_in_rows(q):
                 for a in range(UNITS[q] // 2):
                     nc.scalar.activation(out=t[:, 2 * a : 2 * a + 2, :], in_=pu_of[(q, a)][:], func=ACT.Tanh)
             else:
@@ -221,7 +256,7 @@ def tile_gatel0rdcell_pa_t_kernel(tc, x_t, h_tminus1, gate_noise, Wg, bg, Wr, br
                     nc.vector.tensor_tensor(
                         out=u[:, 2 * a : 2 * a + 2, :],
                         in0=pu_of[(q, a)][:],
-                        in1=nz_of[q][:, 2 * a : 2 * a + 2, :],
+                        in1=nb_of[q][:, 2 * a : 2 * a + 2, :],
                         op=ALU.subtract,
                     )
                 nc.scalar.activation(out=t[:], in_=u[:], func=ACT.Tanh)
@@ -240,15 +275,9 @@ def tile_gatel0rdcell_pa_t_kernel(tc, x_t, h_tminus1, gate_noise, Wg, bg, Wr, br
 
         def gated(q):
             lam = opool.tile([P, UNITS[q], D], F32)
-            for a in range(UNITS[q] // 2):
-                nc.gpsimd.tensor_scalar(
-                    out=lam[:, 2 * a : 2 * a + 2, :],
-                    in0=t_of[q][:, 2 * a : 2 * a + 2, :],
-                    scalar1=0.0,
-                    scalar2=0.0,
-                    op0=ALU.max,
-                    op1=ALU.add,
-                )
+            nc.vector.tensor_scalar_max(out=lam[:, 0:2, :], in0=t_of[q][:, 0:2, :], scalar1=0.0)
+            if UNITS[q] == 4:
+                nc.scalar.activation(out=lam[:, 2:4, :], in_=t_of[q][:, 2:4, :], func=ACT.Relu)
             nc.sync.dma_start(out=o1v[:, rows_of(q), :], in_=lam[:])
             d = d_of[q]
             nc.vector.scalar_tensor_tensor(out=d[:], in0=t_of[q][:], scalar=0.0, in1=d[:], op0=ALU.max, op1=ALU.mult)
@@ -262,26 +291,33 @@ def tile_gatel0rdcell_pa_t_kernel(tc, x_t, h_tminus1, gate_noise, Wg, bg, Wr, br
             return 0 <= q < NU
 
         def body():
+            noise_bias(0)
             for it in range(-1, NU + 2):
                 if it >= 0 and on(it + LOOKAHEAD):
                     load_g(it + LOOKAHEAD)
                 if it >= 0 and on(it + LOOKAHEAD - 1):
                     load_n(it + LOOKAHEAD - 1)
+                if on(it + 2) and gate_in_rows(it + 2):
+                    noise_bias(it + 2)
                 if on(it):
                     mx(it, 2)
                     tanh_r(it)
-                if on(it - 2):
+                if on(it - 2) and not gate_in_rows(it - 2):
                     tanh_i(it - 2)
                 if on(it - 1):
                     diff(it - 1)
                 if on(it + 1):
                     g_transposes(it + 1)
                     g_evacuate(it + 1)
-                if on(it):
+                if on(it) and gate_in_rows(it):
+                    mx_gate_rows(it)
+                    tanh_i(it)
+                    back_r(it)
+                if on(it) and not gate_in_rows(it):
                     mx(it, 0)
                     bias_i(it)
                     back_r(it)
-                if on(it - 1):
+                if on(it - 1) and not gate_in_rows(it - 1):
                     back_i(it - 1)
                 if on(it - 2):
                     gated(it - 2)

@@ -18,12 +18,12 @@ D = 256
 NT = 64
 UNITS = (2, 2, 4, 4, 4, 4, 4, 4, 4, 4, 4, 4, 4, 4, 4, 4, 2, 2)
 NU = 18
-LOOKAHEAD = 4
-MANUAL = False
+LOOKAHEAD = 5
+GT_BANKS, PT_BANKS, PH_BANKS, PU_BANKS = 2, 2, 2, 2
 
 
-def gate_in_rows(q):
-    return q < 5
+def noise_on_vector(pair):
+    return pair % 4 == 1 and pair < 28
 
 
 def tile_gatel0rdcell_pa_t_kernel(tc, x_t, h_tminus1, gate_noise, Wg, bg, Wr, br, out_0, out_1):
@@ -38,17 +38,16 @@ def tile_gatel0rdcell_pa_t_kernel(tc, x_t, h_tminus1, gate_noise, Wg, bg, Wr, br
 
     with ExitStack() as ctx:
         const = ctx.enter_context(tc.tile_pool(name="const", bufs=1))
-        gpool = ctx.enter_context(tc.tile_pool(name="gpool", bufs=LOOKAHEAD + 4))
-        npool = ctx.enter_context(tc.tile_pool(name="npool", bufs=LOOKAHEAD + 3))
+        gpool = ctx.enter_context(tc.tile_pool(name="gpool", bufs=LOOKAHEAD + 5))
+        npool = ctx.enter_context(tc.tile_pool(name="npool", bufs=LOOKAHEAD + 4))
         grpool = ctx.enter_context(tc.tile_pool(name="grpool", bufs=4))
-        cpool = ctx.enter_context(tc.tile_pool(name="cpool", bufs=3))
+        cpool = ctx.enter_context(tc.tile_pool(name="cpool", bufs=4))
         hpool = ctx.enter_context(tc.tile_pool(name="hpool", bufs=4))
         ipool = ctx.enter_context(tc.tile_pool(name="ipool", bufs=6))
         upool = ctx.enter_context(tc.tile_pool(name="upool", bufs=2))
-        nbpool = ctx.enter_context(tc.tile_pool(name="nbpool", bufs=5))
-        tpool = ctx.enter_context(tc.tile_pool(name="tpool", bufs=3))
-        dpool = ctx.enter_context(tc.tile_pool(name="dpool", bufs=3))
-        opool = ctx.enter_context(tc.tile_pool(name="opool", bufs=3))
+        tpool = ctx.enter_context(tc.tile_pool(name="tpool", bufs=4))
+        dpool = ctx.enter_context(tc.tile_pool(name="dpool", bufs=4))
+        opool = ctx.enter_context(tc.tile_pool(name="opool", bufs=4))
         psum = ctx.enter_context(tc.psum_pool(name="psum", bufs=2))
 
         g_of = {}
@@ -64,6 +63,7 @@ def tile_gatel0rdcell_pa_t_kernel(tc, x_t, h_tminus1, gate_noise, Wg, bg, Wr, br
         pu_of = {}
         t_of = {}
         d_of = {}
+        lam_of = {}
 
         def rows_of(q):
             return slice(FIRST[q], FIRST[q] + UNITS[q])
@@ -79,206 +79,167 @@ def tile_gatel0rdcell_pa_t_kernel(tc, x_t, h_tminus1, gate_noise, Wg, bg, Wr, br
             nc.sync.dma_start(out=nz[:], in_=nv[:, rows_of(q), :])
             nz_of[q] = nz
 
-        bg_row = const.tile([P, D], BF16)
-        nc.vector.memset(bg_row[:], 0.0)
-        nc.scalar.dma_start(out=bg_row[0:1, :], in_=bg.rearrange("(o n) -> o n", o=1))
-        ones = const.tile([P, P], BF16)
-        nc.vector.memset(ones[:], 1.0)
-        bg_ps = psum.tile([P, 2, D], F32, tag="pu")
-        nc.tensor.matmul(out=bg_ps[:, 0, :], lhsT=ones[:], rhs=bg_row[:], start=True, stop=True)
-        bg_b = const.tile([P, D], F32)
-        nc.vector.tensor_copy(out=bg_b[:], in_=bg_ps[:, 0, :])
-        nb_of = {}
-
-        def noise_bias(q):
-            nb = nbpool.tile([P, UNITS[q], D], F32)
-            nc.vector.tensor_tensor(
-                out=nb[:], in0=nz_of[q][:], in1=bg_b[:].unsqueeze(1).to_broadcast([P, UNITS[q], D]), op=ALU.subtract
-            )
-            nb_of[q] = nb
-
-        load_g(0)
-        for q in range(1, LOOKAHEAD):
-            load_n(q - 1)
-            load_g(q)
-
-        warm = const.tile([P, 1], F32)
-        nc.vector.memset(warm[:], 0.0)
-        nc.scalar.activation(out=warm[:], in_=warm[:], func=ACT.Tanh)
-
         b_rows = const.tile([P, P], BF16)
         nc.vector.memset(b_rows[:], 0.0)
+        warm = const.tile([P, 1], F32)
+        nc.vector.memset(warm[:], 0.0)
         nc.scalar.dma_start(out=b_rows[0:2, :], in_=bg.rearrange("(f p) -> f p", p=P))
         nc.scalar.dma_start(out=b_rows[2:4, :], in_=br.rearrange("(f p) -> f p", p=P))
-        w_raw = const.tile([P, 2, 4, D], BF16)
-        nc.scalar.dma_start(out=w_raw[:, 0], in_=Wg.rearrange("(p j) w -> p j w", j=4))
-        nc.scalar.dma_start(out=w_raw[:, 1], in_=Wr.rearrange("(p j) w -> p j w", j=4))
+        nc.scalar.activation(out=warm[:], in_=warm[:], func=ACT.Tanh)
 
         ident = const.tile([P, P], F32)
         make_identity(nc, ident[:])
-        neg_ident = const.tile([P, P], BF16)
-        nc.vector.tensor_scalar_mul(out=neg_ident[:], in0=ident[:], scalar1=-1.0)
+        w_raw = const.tile([P, 2, 4, D], BF16)
+        load_g(0)
+        nc.sync.dma_start(out=w_raw[:, 1], in_=Wr.rearrange("(p j) w -> p j w", j=4))
+        nc.sync.dma_start(out=w_raw[:, 0], in_=Wg.rearrange("(p j) w -> p j w", j=4))
+        for q in range(1, LOOKAHEAD):
+            load_g(q)
+            load_n(q - 1)
 
         w_grp = const.tile([P, 2, D, 4], BF16, align_bytes=64)
-        for m in range(2):
-            nc.vector.tensor_copy(out=w_grp[:, m], in_=w_raw[:, m].rearrange("p j w -> p w j"))
         w_codes = const.tile([P, 2 * D], U32, align_bytes=64)
         w_scales = const.tile([P, 2 * D], U8, align_bytes=64)
-        nc.vector.quantize_mx(
-            out=w_codes[:].bitcast(FP8X4),
-            scales=w_scales[:],
-            in_=w_grp[:].rearrange("p m w j -> p (m w j)"),
-        )
 
-        b_f32 = const.tile([P, P], F32)
-        nc.vector.tensor_copy(out=b_f32[:], in_=b_rows[:])
-        b_ps = psum.tile([P, 2, D], F32, tag="ph")
-        nc.tensor.transpose(b_ps[:, 0, 0:P], b_f32[:], ident[:])
-        b_col = const.tile([P, 4], F32)
-        nc.vector.tensor_copy(out=b_col[:], in_=b_ps[:, 0, 0:4])
+        def weights(m):
+            nc.vector.tensor_copy(out=w_grp[:, m], in_=w_raw[:, m].rearrange("p j w -> p w j"))
+            cols = slice(m * D, (m + 1) * D)
+            nc.vector.quantize_mx(
+                out=w_codes[:, cols].bitcast(FP8X4),
+                scales=w_scales[:, cols],
+                in_=w_grp[:, m].rearrange("p w j -> p (w j)"),
+            )
 
-        def g_transposes(q):
+        weights(1)
+        neg_ident = const.tile([P, P], BF16)
+        nc.vector.tensor_scalar_mul(out=neg_ident[:], in0=ident[:], scalar1=-1.0)
+        def g_transposes(q, a):
             gw = g_of[q][:].bitcast(F32).rearrange("p t (j e) -> p t e j", e=2)
-            for a in range(UNITS[q] // 2):
-                gt = psum.tile([P, 2, 2, P], F32, tag="gt")
-                for i in range(2):
-                    for e in range(2):
-                        nc.tensor.transpose(gt[:, e, i, :], gw[:, 2 * a + i, e, :], ident[:])
-                gt_of[(q, a)] = gt
+            gt = psum.tile([P, 2, 2, P], F32, tag="gt", bufs=GT_BANKS)
+            for i in range(2):
+                for e in range(2):
+                    nc.tensor.transpose(gt[:, e, i, :], gw[:, 2 * a + i, e, :], ident[:])
+            gt_of[(q, a)] = gt
 
-        def g_evacuate(q):
-            for a in range(UNITS[q] // 2):
-                gr = grpool.tile([P, 4 * 2 * P], BF16, align_bytes=64)
-                nc.scalar.copy(
-                    out=gr[:].bitcast(F32).rearrange("p (c e) -> p c e", e=2),
-                    in_=gt_of[(q, a)][:].rearrange("p e i l -> p (i l) e"),
-                )
-                gr_of[(q, a)] = gr
+        def g_evacuate(q, a):
+            gr = grpool.tile([P, 4 * 2 * P], BF16, align_bytes=64)
+            nc.scalar.copy(
+                out=gr[:].bitcast(F32).rearrange("p (c e) -> p c e", e=2),
+                in_=gt_of[(q, a)][:].rearrange("p e i l -> p (i l) e"),
+            )
+            gr_of[(q, a)] = gr
 
-        def g_quantise(q):
-            gc = cpool.tile([P, UNITS[q] * P], U32, align_bytes=64)
-            gs = cpool.tile([P, UNITS[q] * P], U8, align_bytes=64)
-            for a in range(UNITS[q] // 2):
-                cols = slice(a * 2 * P, (a + 1) * 2 * P)
-                nc.vector.quantize_mx(out=gc[:, cols].bitcast(FP8X4), scales=gs[:, cols], in_=gr_of[(q, a)][:])
-            gc_of[q] = gc
-            gs_of[q] = gs
+        def g_quantise(q, a):
+            if a == 0:
+                gc_new = cpool.tile([P, UNITS[q] * P], U32, align_bytes=64)
+                gs_new = cpool.tile([P, UNITS[q] * P], U8, align_bytes=64)
+                gc_of[q] = gc_new
+                gs_of[q] = gs_new
+            cols = slice(a * 2 * P, (a + 1) * 2 * P)
+            nc.vector.quantize_mx(
+                out=gc_of[q][:, cols].bitcast(FP8X4), scales=gs_of[q][:, cols], in_=gr_of[(q, a)][:]
+            )
 
-        def mx(q, first):
-            for w in range(first, first + 2):
-                pt = psum.tile([P, UNITS[q] * P], F32, tag="pt")
-                wcols = slice(w * P, (w + 1) * P)
-                nc.tensor.matmul_mx(
-                    out=pt[:],
-                    lhsT=w_codes[:, wcols].bitcast(FP8X4),
-                    lhsT_scale=w_scales[:, wcols],
-                    rhs=gc_of[q][:].bitcast(FP8X4),
-                    rhs_scale=gs_of[q][:],
-                    start=True,
-                    stop=True,
-                )
-                pt_of[(q, w)] = pt
+        def mx(q, w):
+            pt = psum.tile([P, UNITS[q] * P], F32, tag="pt", bufs=PT_BANKS)
+            wcols = slice(w * P, (w + 1) * P)
+            nc.tensor.matmul_mx(
+                out=pt[:],
+                lhsT=w_codes[:, wcols].bitcast(FP8X4),
+                lhsT_scale=w_scales[:, wcols],
+                rhs=gc_of[q][:].bitcast(FP8X4),
+                rhs_scale=gs_of[q][:],
+                start=True,
+                stop=True,
+            )
+            pt_of[(q, w)] = pt
 
-        def mx_gate_rows(q):
-            for a in range(UNITS[q] // 2):
-                pu = psum.tile([P, 2, D], F32, tag="pu")
-                for i in range(2):
-                    cols = slice((2 * a + i) * P, (2 * a + i + 1) * P)
-                    nc.tensor.matmul_mx(
-                        out=pu[:, i, :],
-                        lhsT=gc_of[q][:, cols].bitcast(FP8X4),
-                        lhsT_scale=gs_of[q][:, cols],
-                        rhs=w_codes[:, 0:D].bitcast(FP8X4),
-                        rhs_scale=w_scales[:, 0:D],
-                        start=True,
-                        stop=True,
+        def tanh_r(q, f):
+            hT = hpool.tile([P, UNITS[q] * P], F32)
+            nc.scalar.activation(
+                out=hT[:], in_=pt_of[(q, 2 + f)][:], func=ACT.Tanh, bias=b_col[:, 2 + f : 3 + f], scale=1.0
+            )
+            hT_of[(q, f)] = hT
+
+        def bias_i(q, f):
+            iT = ipool.tile([P, UNITS[q] * P], F32)
+            nc.scalar.activation(
+                out=iT[:], in_=pt_of[(q, f)][:], func=ACT.Identity, bias=b_col[:, f : f + 1], scale=1.0
+            )
+            iT_of[(q, f)] = iT
+
+        def back_r(q, a):
+            ph = psum.tile([P, 2, D], F32, tag="ph", bufs=PH_BANKS)
+            for i in range(2):
+                for f in range(2):
+                    nc.tensor.transpose(
+                        ph[:, i, f * P : (f + 1) * P],
+                        hT_of[(q, f)][:, (2 * a + i) * P : (2 * a + i + 1) * P],
+                        ident[:],
                     )
-                pu_of[(q, a)] = pu
+            ph_of[(q, a)] = ph
 
-        def tanh_r(q):
-            for f in range(2):
-                hT = hpool.tile([P, UNITS[q] * P], F32)
-                nc.scalar.activation(
-                    out=hT[:], in_=pt_of[(q, 2 + f)][:], func=ACT.Tanh, bias=b_col[:, 2 + f : 3 + f], scale=1.0
+        def back_i(q, a):
+            alone = noise_on_vector(FIRST[q] // 2 + a)
+            pu = psum.tile([P, 2, D], F32, tag="pu", bufs=PU_BANKS)
+            if not alone:
+                nc.tensor.matmul(
+                    out=pu[:], lhsT=neg_ident[:], rhs=nz_of[q][:, 2 * a : 2 * a + 2, :], start=True, stop=False
                 )
-                hT_of[(q, f)] = hT
-
-        def bias_i(q):
-            for f in range(2):
-                iT = ipool.tile([P, UNITS[q] * P], F32)
-                nc.scalar.activation(
-                    out=iT[:], in_=pt_of[(q, f)][:], func=ACT.Identity, bias=b_col[:, f : f + 1], scale=1.0
-                )
-                iT_of[(q, f)] = iT
-
-        def back_r(q):
-            for a in range(UNITS[q] // 2):
-                ph = psum.tile([P, 2, D], F32, tag="ph")
-                for i in range(2):
-                    for f in range(2):
-                        nc.tensor.transpose(
-                            ph[:, i, f * P : (f + 1) * P],
-                            hT_of[(q, f)][:, (2 * a + i) * P : (2 * a + i + 1) * P],
-                            ident[:],
-                        )
-                ph_of[(q, a)] = ph
-
-        def back_i(q):
-            sub = True
-            pairs = range(UNITS[q] // 2)
-            for a in pairs:
-                pu = psum.tile([P, 2, D], F32, tag="pu")
-                if sub:
+            for i in range(2):
+                for f in range(2):
                     nc.tensor.matmul(
-                        out=pu[:], lhsT=neg_ident[:], rhs=nz_of[q][:, 2 * a : 2 * a + 2, :], start=True, stop=False
+                        out=pu[:, i, f * P : (f + 1) * P],
+                        lhsT=iT_of[(q, f)][:, (2 * a + i) * P : (2 * a + i + 1) * P],
+                        rhs=ident[:],
+                        is_transpose=True,
+                        start=alone,
+                        stop=(i == 1 and f == 1) or alone,
                     )
-                pu_of[(q, a)] = pu
-            for a in pairs:
-                for i in range(2):
-                    for f in range(2):
-                        nc.tensor.matmul(
-                            out=pu_of[(q, a)][:, i, f * P : (f + 1) * P],
-                            lhsT=iT_of[(q, f)][:, (2 * a + i) * P : (2 * a + i + 1) * P],
-                            rhs=ident[:],
-                            is_transpose=True,
-                            start=not sub,
-                            stop=(i == 1 and f == 1) or not sub,
-                        )
+            pu_of[(q, a)] = pu
 
-        def tanh_i(q):
-            t = tpool.tile([P, UNITS[q], D], F32)
-            if not gate_in_rows(q):
-                for a in range(UNITS[q] // 2):
-                    nc.scalar.activation(out=t[:, 2 * a : 2 * a + 2, :], in_=pu_of[(q, a)][:], func=ACT.Tanh)
-            else:
-                u = upool.tile([P, UNITS[q], D], F32)
-                for a in range(UNITS[q] // 2):
-                    nc.vector.tensor_tensor(
-                        out=u[:, 2 * a : 2 * a + 2, :],
-                        in0=pu_of[(q, a)][:],
-                        in1=nb_of[q][:, 2 * a : 2 * a + 2, :],
-                        op=ALU.subtract,
-                    )
-                nc.scalar.activation(out=t[:], in_=u[:], func=ACT.Tanh)
-            t_of[q] = t
-
-        def diff(q):
-            d = dpool.tile([P, UNITS[q], D], F32)
-            for a in range(UNITS[q] // 2):
+        def subtract_noise(q, a):
+            if noise_on_vector(FIRST[q] // 2 + a):
+                u = upool.tile([P, 2, D], F32)
                 nc.vector.tensor_tensor(
-                    out=d[:, 2 * a : 2 * a + 2, :],
-                    in0=ph_of[(q, a)][:],
-                    in1=g_of[q][:, 2 * a : 2 * a + 2, D : 2 * D],
-                    op=ALU.subtract,
+                    out=u[:], in0=pu_of[(q, a)][:], in1=nz_of[q][:, 2 * a : 2 * a + 2, :], op=ALU.subtract
                 )
-            d_of[q] = d
+                pu_of[(q, a)] = u
 
-        def gated(q):
+        def tanh_i(q, a):
+            if a == 0:
+                t_new = tpool.tile([P, UNITS[q], D], F32)
+                t_of[q] = t_new
+            nc.scalar.activation(out=t_of[q][:, 2 * a : 2 * a + 2, :], in_=pu_of[(q, a)][:], func=ACT.Tanh)
+
+        def diff(q, a):
+            if a == 0:
+                d_new = dpool.tile([P, UNITS[q], D], F32)
+                d_of[q] = d_new
+            two = slice(2 * a, 2 * a + 2)
+            nc.vector.tensor_tensor(
+                out=d_of[q][:, two, :], in0=ph_of[(q, a)][:], in1=g_of[q][:, two, D : 2 * D], op=ALU.subtract
+            )
+
+        def vector_tiles(q):
+            return min(UNITS[q], 3) if q < NU - 3 else 0
+
+        def relu_vector(q):
             lam = opool.tile([P, UNITS[q], D], F32)
-            nc.vector.tensor_scalar_max(out=lam[:, 0:2, :], in0=t_of[q][:, 0:2, :], scalar1=0.0)
-            if UNITS[q] == 4:
-                nc.scalar.activation(out=lam[:, 2:4, :], in_=t_of[q][:, 2:4, :], func=ACT.Relu)
-            nc.sync.dma_start(out=o1v[:, rows_of(q), :], in_=lam[:])
+            lam_of[q] = lam
+            share = vector_tiles(q)
+            if share > 0:
+                nc.vector.tensor_scalar_max(out=lam[:, 0:share, :], in0=t_of[q][:, 0:share, :], scalar1=0.0)
+
+        def relu_scalar(q):
+            share = vector_tiles(q)
+            if UNITS[q] > share:
+                nc.scalar.activation(out=lam_of[q][:, share:, :], in_=t_of[q][:, share:, :], func=ACT.Relu)
+
+        def store_gate(q):
+            nc.sync.dma_start(out=o1v[:, rows_of(q), :], in_=lam_of[q][:])
+
+        def gate(q):
             d = d_of[q]
             nc.vector.scalar_tensor_tensor(out=d[:], in0=t_of[q][:], scalar=0.0, in1=d[:], op0=ALU.max, op1=ALU.mult)
 
@@ -287,47 +248,109 @@ def tile_gatel0rdcell_pa_t_kernel(tc, x_t, h_tminus1, gate_noise, Wg, bg, Wr, br
             nc.vector.tensor_tensor(out=ht[:], in0=d_of[q][:], in1=g_of[q][:, :, D : 2 * D], op=ALU.add)
             nc.sync.dma_start(out=o0v[:, rows_of(q), :], in_=ht[:])
 
+        b_col = const.tile([P, 4], F32)
+
+        def bias_columns():
+            b_f32 = const.tile([P, P], F32)
+            nc.vector.tensor_copy(out=b_f32[:], in_=b_rows[:])
+            b_ps = psum.tile([P, 2, D], F32, tag="ph")
+            nc.tensor.transpose(b_ps[:, 0, 0:P], b_f32[:], ident[:])
+            nc.vector.tensor_copy(out=b_col[:], in_=b_ps[:, 0, 0:4])
+
         def on(q):
             return 0 <= q < NU
 
-        def body():
-            noise_bias(0)
-            for it in range(-1, NU + 2):
-                if it >= 0 and on(it + LOOKAHEAD):
-                    load_g(it + LOOKAHEAD)
-                if it >= 0 and on(it + LOOKAHEAD - 1):
-                    load_n(it + LOOKAHEAD - 1)
-                if on(it + 2) and gate_in_rows(it + 2):
-                    noise_bias(it + 2)
-                if on(it):
-                    mx(it, 2)
-                    tanh_r(it)
-                if on(it - 2) and not gate_in_rows(it - 2):
-                    tanh_i(it - 2)
-                if on(it - 1):
-                    diff(it - 1)
-                if on(it + 1):
-                    g_transposes(it + 1)
-                    g_evacuate(it + 1)
-                if on(it) and gate_in_rows(it):
-                    mx_gate_rows(it)
-                    tanh_i(it)
-                    back_r(it)
-                if on(it) and not gate_in_rows(it):
-                    mx(it, 0)
-                    bias_i(it)
-                    back_r(it)
-                if on(it - 1) and not gate_in_rows(it - 1):
-                    back_i(it - 1)
-                if on(it - 2):
-                    gated(it - 2)
-                if on(it + 1):
-                    g_quantise(it + 1)
-                if on(it - 2):
-                    outputs(it - 2)
+        def pairs(q):
+            return range(UNITS[q] // 2)
 
-        if MANUAL:
-            with tc.manual_schedule():
-                body()
-        else:
-            body()
+        def step(k):
+            q = k + 0
+            if on(q):
+                mx(q, 2)
+                mx(q, 3)
+            q = k + 0
+            if on(q):
+                tanh_r(q, 0)
+            q = k + 0
+            if on(q):
+                tanh_r(q, 1)
+            q = k + 2
+            if on(q):
+                g_transposes(q, 0)
+            q = k + 2
+            if on(q):
+                g_evacuate(q, 0)
+            q = k + 2
+            if on(q) and UNITS[q] == 4:
+                g_transposes(q, 1)
+            q = k + 2
+            if on(q) and UNITS[q] == 4:
+                g_evacuate(q, 1)
+            q = k + 0
+            if on(q):
+                mx(q, 0)
+                mx(q, 1)
+            q = k + 0
+            if on(q):
+                bias_i(q, 0)
+            q = k + 0
+            if on(q):
+                bias_i(q, 1)
+            q = k - 1
+            if on(q):
+                back_r(q, 0)
+            q = k - 1
+            if on(q) and UNITS[q] == 4:
+                back_r(q, 1)
+            q = k + 1
+            if on(q):
+                for a in pairs(q):
+                    g_quantise(q, a)
+            q = k - 2
+            if on(q):
+                relu_vector(q)
+            q = k - 2
+            if on(q):
+                gate(q)
+            q = k - 1
+            if on(q):
+                diff(q, 0)
+            q = k - 1
+            if on(q) and UNITS[q] == 4:
+                diff(q, 1)
+            q = k - 1
+            if on(q):
+                back_i(q, 0)
+            q = k - 1
+            if on(q) and UNITS[q] == 4:
+                back_i(q, 1)
+            q = k - 1
+            if on(q):
+                subtract_noise(q, 0)
+            q = k - 1
+            if on(q) and UNITS[q] == 4:
+                subtract_noise(q, 1)
+            q = k - 2
+            if on(q):
+                outputs(q)
+            q = k - 2
+            if on(q):
+                relu_scalar(q)
+                store_gate(q)
+            q = k - 1
+            if on(q):
+                tanh_i(q, 0)
+            q = k - 1
+            if on(q) and UNITS[q] == 4:
+                tanh_i(q, 1)
+
+        with tc.manual_schedule():
+            for k in range(-2, NU + 2):
+                if k >= 0 and on(k + LOOKAHEAD):
+                    load_g(k + LOOKAHEAD)
+                if k >= 0 and on(k + LOOKAHEAD - 1):
+                    load_n(k + LOOKAHEAD - 1)
+                step(k)
+                if k == -1:
+                    bias_columns()
+                    weights(0)

@@ -268,6 +268,18 @@ def tile_gatel0rdcell_pa_t_kernel(tc, x_t, h_tminus1, gate_noise, Wg, bg, Wr, br
             if on(q):
                 mx(q, 2)
                 mx(q, 3)
+            q = k + 2
+            if on(q):
+                g_transposes(q, 0)
+            q = k - 1
+            if on(q):
+                back_r(q, 0)
+            q = k - 1
+            if on(q):
+                back_i(q, 0)
+            q = k - 1
+            if on(q):
+                subtract_noise(q, 0)
             q = k + 0
             if on(q):
                 tanh_r(q, 0)
@@ -276,32 +288,7 @@ def tile_gatel0rdcell_pa_t_kernel(tc, x_t, h_tminus1, gate_noise, Wg, bg, Wr, br
                 tanh_r(q, 1)
             q = k + 2
             if on(q):
-                g_transposes(q, 0)
-            q = k + 2
-            if on(q):
                 g_evacuate(q, 0)
-            q = k + 2
-            if on(q) and UNITS[q] == 4:
-                g_transposes(q, 1)
-            q = k + 2
-            if on(q) and UNITS[q] == 4:
-                g_evacuate(q, 1)
-            q = k + 0
-            if on(q):
-                mx(q, 0)
-                mx(q, 1)
-            q = k + 0
-            if on(q):
-                bias_i(q, 0)
-            q = k + 0
-            if on(q):
-                bias_i(q, 1)
-            q = k - 1
-            if on(q):
-                back_r(q, 0)
-            q = k - 1
-            if on(q) and UNITS[q] == 4:
-                back_r(q, 1)
             q = k + 1
             if on(q):
                 for a in pairs(q):
@@ -311,38 +298,51 @@ def tile_gatel0rdcell_pa_t_kernel(tc, x_t, h_tminus1, gate_noise, Wg, bg, Wr, br
                 relu_vector(q)
             q = k - 2
             if on(q):
+                relu_scalar(q)
+                store_gate(q)
+            q = k - 2
+            if on(q):
                 gate(q)
             q = k - 1
             if on(q):
                 diff(q, 0)
+            q = k + 0
+            if on(q):
+                mx(q, 0)
+                mx(q, 1)
+            q = k + 2
+            if on(q) and UNITS[q] == 4:
+                g_transposes(q, 1)
             q = k - 1
             if on(q) and UNITS[q] == 4:
-                diff(q, 1)
-            q = k - 1
-            if on(q):
-                back_i(q, 0)
+                back_r(q, 1)
             q = k - 1
             if on(q) and UNITS[q] == 4:
                 back_i(q, 1)
             q = k - 1
-            if on(q):
-                subtract_noise(q, 0)
-            q = k - 1
             if on(q) and UNITS[q] == 4:
                 subtract_noise(q, 1)
-            q = k - 2
+            q = k + 0
             if on(q):
-                outputs(q)
-            q = k - 2
+                bias_i(q, 0)
+            q = k + 0
             if on(q):
-                relu_scalar(q)
-                store_gate(q)
+                bias_i(q, 1)
             q = k - 1
             if on(q):
                 tanh_i(q, 0)
+            q = k + 2
+            if on(q) and UNITS[q] == 4:
+                g_evacuate(q, 1)
             q = k - 1
             if on(q) and UNITS[q] == 4:
                 tanh_i(q, 1)
+            q = k - 1
+            if on(q) and UNITS[q] == 4:
+                diff(q, 1)
+            q = k - 2
+            if on(q):
+                outputs(q)
 
         with tc.manual_schedule():
             for k in range(-2, NU + 2):

@@ -222,7 +222,7 @@ def tile_gatel0rdcell_pa_t_kernel(tc, x_t, h_tminus1, gate_noise, Wg, bg, Wr, br
             )
 
         def vector_tiles(q):
-            return min(UNITS[q], 3) if q < NU - 3 else 0
+            return UNITS[q] if q < NU - 4 else 0
 
         def relu_vector(q):
             lam = opool.tile([P, UNITS[q], D], F32)
@@ -245,7 +245,14 @@ def tile_gatel0rdcell_pa_t_kernel(tc, x_t, h_tminus1, gate_noise, Wg, bg, Wr, br
 
         def outputs(q):
             ht = opool.tile([P, UNITS[q], D], F32)
-            nc.vector.tensor_tensor(out=ht[:], in0=d_of[q][:], in1=g_of[q][:, :, D : 2 * D], op=ALU.add)
+            mine = UNITS[q] - 1 if q < NU - 3 and UNITS[q] == 4 else UNITS[q]
+            for i in range(mine, UNITS[q]):
+                nc.gpsimd.tensor_tensor(
+                    out=ht[:, i, :], in0=d_of[q][:, i, :], in1=g_of[q][:, i, D : 2 * D], op=ALU.add
+                )
+            nc.vector.tensor_tensor(
+                out=ht[:, 0:mine, :], in0=d_of[q][:, 0:mine, :], in1=g_of[q][:, 0:mine, D : 2 * D], op=ALU.add
+            )
             nc.sync.dma_start(out=o0v[:, rows_of(q), :], in_=ht[:])
 
         b_col = const.tile([P, 4], F32)

@@ -22,7 +22,7 @@ LOOKAHEAD = 5
 GT_BANKS, PT_BANKS, PH_BANKS, PU_BANKS = 2, 2, 2, 2
 
 
-def noise_on_vector(pair):
+def h_on_vector(pair):
     return pair % 4 == 1 and pair < 28
 
 
@@ -39,14 +39,15 @@ def tile_gatel0rdcell_pa_t_kernel(tc, x_t, h_tminus1, gate_noise, Wg, bg, Wr, br
     with ExitStack() as ctx:
         const = ctx.enter_context(tc.tile_pool(name="const", bufs=1))
         gpool = ctx.enter_context(tc.tile_pool(name="gpool", bufs=LOOKAHEAD + 5))
-        npool = ctx.enter_context(tc.tile_pool(name="npool", bufs=LOOKAHEAD + 4))
+        npool = ctx.enter_context(tc.tile_pool(name="npool", bufs=LOOKAHEAD + 2))
         grpool = ctx.enter_context(tc.tile_pool(name="grpool", bufs=4))
         cpool = ctx.enter_context(tc.tile_pool(name="cpool", bufs=4))
         hpool = ctx.enter_context(tc.tile_pool(name="hpool", bufs=4))
-        ipool = ctx.enter_context(tc.tile_pool(name="ipool", bufs=6))
-        upool = ctx.enter_context(tc.tile_pool(name="upool", bufs=2))
-        tpool = ctx.enter_context(tc.tile_pool(name="tpool", bufs=4))
-        dpool = ctx.enter_context(tc.tile_pool(name="dpool", bufs=4))
+        nbpool = ctx.enter_context(tc.tile_pool(name="nbpool", bufs=2))
+        upool = ctx.enter_context(tc.tile_pool(name="upool", bufs=3))
+        tpool = ctx.enter_context(tc.tile_pool(name="tpool", bufs=3))
+        dpool = ctx.enter_context(tc.tile_pool(name="dpool", bufs=3))
+        epool = ctx.enter_context(tc.tile_pool(name="epool", bufs=3))
         opool = ctx.enter_context(tc.tile_pool(name="opool", bufs=4))
         psum = ctx.enter_context(tc.psum_pool(name="psum", bufs=2))
 
@@ -58,11 +59,12 @@ def tile_gatel0rdcell_pa_t_kernel(tc, x_t, h_tminus1, gate_noise, Wg, bg, Wr, br
         gs_of = {}
         pt_of = {}
         hT_of = {}
-        iT_of = {}
         ph_of = {}
         pu_of = {}
+        nb_of = {}
+        u_of = {}
         t_of = {}
-        d_of = {}
+        e_of = {}
         lam_of = {}
 
         def rows_of(q):
@@ -81,10 +83,14 @@ def tile_gatel0rdcell_pa_t_kernel(tc, x_t, h_tminus1, gate_noise, Wg, bg, Wr, br
 
         b_rows = const.tile([P, P], BF16)
         nc.vector.memset(b_rows[:], 0.0)
+        bg_row = const.tile([P, D], BF16)
+        nc.vector.memset(bg_row[:], 0.0)
         warm = const.tile([P, 1], F32)
         nc.vector.memset(warm[:], 0.0)
-        nc.scalar.dma_start(out=b_rows[0:2, :], in_=bg.rearrange("(f p) -> f p", p=P))
-        nc.scalar.dma_start(out=b_rows[2:4, :], in_=br.rearrange("(f p) -> f p", p=P))
+        ones = const.tile([P, P], BF16)
+        nc.vector.memset(ones[:], 1.0)
+        nc.scalar.dma_start(out=b_rows[0:2, :], in_=br.rearrange("(f p) -> f p", p=P))
+        nc.scalar.dma_start(out=bg_row[0:1, :], in_=bg.rearrange("(o n) -> o n", o=1))
         nc.scalar.activation(out=warm[:], in_=warm[:], func=ACT.Tanh)
 
         ident = const.tile([P, P], F32)
@@ -94,8 +100,8 @@ def tile_gatel0rdcell_pa_t_kernel(tc, x_t, h_tminus1, gate_noise, Wg, bg, Wr, br
         nc.sync.dma_start(out=w_raw[:, 1], in_=Wr.rearrange("(p j) w -> p j w", j=4))
         nc.sync.dma_start(out=w_raw[:, 0], in_=Wg.rearrange("(p j) w -> p j w", j=4))
         for q in range(1, LOOKAHEAD):
-            load_g(q)
             load_n(q - 1)
+            load_g(q)
 
         w_grp = const.tile([P, 2, D, 4], BF16, align_bytes=64)
         w_codes = const.tile([P, 2 * D], U32, align_bytes=64)
@@ -113,6 +119,19 @@ def tile_gatel0rdcell_pa_t_kernel(tc, x_t, h_tminus1, gate_noise, Wg, bg, Wr, br
         weights(1)
         neg_ident = const.tile([P, P], BF16)
         nc.vector.tensor_scalar_mul(out=neg_ident[:], in0=ident[:], scalar1=-1.0)
+        br_col = const.tile([P, 2], F32)
+        bg_b = const.tile([P, D], F32)
+
+        def biases():
+            bg_ps = psum.tile([P, 2, D], F32, tag="pu")
+            nc.tensor.matmul(out=bg_ps[:, 0, :], lhsT=ones[:], rhs=bg_row[:], start=True, stop=True)
+            nc.vector.tensor_copy(out=bg_b[:], in_=bg_ps[:, 0, :])
+            b_f32 = const.tile([P, P], F32)
+            nc.vector.tensor_copy(out=b_f32[:], in_=b_rows[:])
+            b_ps = psum.tile([P, 2, D], F32, tag="ph")
+            nc.tensor.transpose(b_ps[:, 0, 0:P], b_f32[:], ident[:])
+            nc.vector.tensor_copy(out=br_col[:], in_=b_ps[:, 0, 0:2])
+
         def g_transposes(q, a):
             gw = g_of[q][:].bitcast(F32).rearrange("p t (j e) -> p t e j", e=2)
             gt = psum.tile([P, 2, 2, P], F32, tag="gt", bufs=GT_BANKS)
@@ -140,9 +159,9 @@ def tile_gatel0rdcell_pa_t_kernel(tc, x_t, h_tminus1, gate_noise, Wg, bg, Wr, br
                 out=gc_of[q][:, cols].bitcast(FP8X4), scales=gs_of[q][:, cols], in_=gr_of[(q, a)][:]
             )
 
-        def mx(q, w):
+        def mx_r(q, f):
             pt = psum.tile([P, UNITS[q] * P], F32, tag="pt", bufs=PT_BANKS)
-            wcols = slice(w * P, (w + 1) * P)
+            wcols = slice(D + f * P, D + (f + 1) * P)
             nc.tensor.matmul_mx(
                 out=pt[:],
                 lhsT=w_codes[:, wcols].bitcast(FP8X4),
@@ -152,77 +171,103 @@ def tile_gatel0rdcell_pa_t_kernel(tc, x_t, h_tminus1, gate_noise, Wg, bg, Wr, br
                 start=True,
                 stop=True,
             )
-            pt_of[(q, w)] = pt
+            pt_of[(q, f)] = pt
+
+        def mx_gate(q, a):
+            pu = psum.tile([P, 2, D], F32, tag="pu", bufs=PU_BANKS)
+            for i in range(2):
+                cols = slice((2 * a + i) * P, (2 * a + i + 1) * P)
+                nc.tensor.matmul_mx(
+                    out=pu[:, i, :],
+                    lhsT=gc_of[q][:, cols].bitcast(FP8X4),
+                    lhsT_scale=gs_of[q][:, cols],
+                    rhs=w_codes[:, 0:D].bitcast(FP8X4),
+                    rhs_scale=w_scales[:, 0:D],
+                    start=True,
+                    stop=True,
+                )
+            pu_of[(q, a)] = pu
 
         def tanh_r(q, f):
             hT = hpool.tile([P, UNITS[q] * P], F32)
             nc.scalar.activation(
-                out=hT[:], in_=pt_of[(q, 2 + f)][:], func=ACT.Tanh, bias=b_col[:, 2 + f : 3 + f], scale=1.0
+                out=hT[:], in_=pt_of[(q, f)][:], func=ACT.Tanh, bias=br_col[:, f : f + 1], scale=1.0
             )
             hT_of[(q, f)] = hT
 
-        def bias_i(q, f):
-            iT = ipool.tile([P, UNITS[q] * P], F32)
-            nc.scalar.activation(
-                out=iT[:], in_=pt_of[(q, f)][:], func=ACT.Identity, bias=b_col[:, f : f + 1], scale=1.0
+        def noise_bias(q):
+            nb = nbpool.tile([P, UNITS[q], D], F32)
+            for i in range(0, UNITS[q], 2):
+                n = 2
+                nc.gpsimd.tensor_tensor(
+                    out=nb[:, i : i + n, :],
+                    in0=nz_of[q][:, i : i + n, :],
+                    in1=bg_b[:].unsqueeze(1).to_broadcast([P, n, D]),
+                    op=ALU.subtract,
+                )
+            nb_of[q] = nb
+
+        def add_i(q, a):
+            if a == 0:
+                u_new = upool.tile([P, UNITS[q], D], F32)
+                u_of[q] = u_new
+            two = slice(2 * a, 2 * a + 2)
+            nc.vector.tensor_tensor(
+                out=u_of[q][:, two, :], in0=pu_of[(q, a)][:], in1=nb_of[q][:, two, :], op=ALU.subtract
             )
-            iT_of[(q, f)] = iT
+
+        def tanh_i(q):
+            t = tpool.tile([P, UNITS[q], D], F32)
+            nc.scalar.activation(out=t[:], in_=u_of[q][:], func=ACT.Tanh)
+            t_of[q] = t
 
         def back_r(q, a):
+            alone = h_on_vector(FIRST[q] // 2 + a)
             ph = psum.tile([P, 2, D], F32, tag="ph", bufs=PH_BANKS)
-            for i in range(2):
-                for f in range(2):
-                    nc.tensor.transpose(
-                        ph[:, i, f * P : (f + 1) * P],
-                        hT_of[(q, f)][:, (2 * a + i) * P : (2 * a + i + 1) * P],
-                        ident[:],
-                    )
-            ph_of[(q, a)] = ph
-
-        def back_i(q, a):
-            alone = noise_on_vector(FIRST[q] // 2 + a)
-            pu = psum.tile([P, 2, D], F32, tag="pu", bufs=PU_BANKS)
             if not alone:
                 nc.tensor.matmul(
-                    out=pu[:], lhsT=neg_ident[:], rhs=nz_of[q][:, 2 * a : 2 * a + 2, :], start=True, stop=False
+                    out=ph[:],
+                    lhsT=neg_ident[:],
+                    rhs=g_of[q][:, 2 * a : 2 * a + 2, D : 2 * D],
+                    start=True,
+                    stop=False,
                 )
             for i in range(2):
                 for f in range(2):
                     nc.tensor.matmul(
-                        out=pu[:, i, f * P : (f + 1) * P],
-                        lhsT=iT_of[(q, f)][:, (2 * a + i) * P : (2 * a + i + 1) * P],
+                        out=ph[:, i, f * P : (f + 1) * P],
+                        lhsT=hT_of[(q, f)][:, (2 * a + i) * P : (2 * a + i + 1) * P],
                         rhs=ident[:],
                         is_transpose=True,
                         start=alone,
                         stop=(i == 1 and f == 1) or alone,
                     )
-            pu_of[(q, a)] = pu
+            ph_of[(q, a)] = ph
 
-        def subtract_noise(q, a):
-            if noise_on_vector(FIRST[q] // 2 + a):
-                u = upool.tile([P, 2, D], F32)
+        def subtract_h(q, a):
+            if h_on_vector(FIRST[q] // 2 + a):
+                d = dpool.tile([P, 2, D], F32)
                 nc.vector.tensor_tensor(
-                    out=u[:], in0=pu_of[(q, a)][:], in1=nz_of[q][:, 2 * a : 2 * a + 2, :], op=ALU.subtract
+                    out=d[:], in0=ph_of[(q, a)][:], in1=g_of[q][:, 2 * a : 2 * a + 2, D : 2 * D], op=ALU.subtract
                 )
-                pu_of[(q, a)] = u
+                ph_of[(q, a)] = d
 
-        def tanh_i(q, a):
+        def gate(q, a):
             if a == 0:
-                t_new = tpool.tile([P, UNITS[q], D], F32)
-                t_of[q] = t_new
-            nc.scalar.activation(out=t_of[q][:, 2 * a : 2 * a + 2, :], in_=pu_of[(q, a)][:], func=ACT.Tanh)
-
-        def diff(q, a):
-            if a == 0:
-                d_new = dpool.tile([P, UNITS[q], D], F32)
-                d_of[q] = d_new
+                e_new = epool.tile([P, UNITS[q], D], F32)
+                e_of[q] = e_new
             two = slice(2 * a, 2 * a + 2)
-            nc.vector.tensor_tensor(
-                out=d_of[q][:, two, :], in0=ph_of[(q, a)][:], in1=g_of[q][:, two, D : 2 * D], op=ALU.subtract
+            nc.vector.scalar_tensor_tensor(
+                out=e_of[q][:, two, :],
+                in0=t_of[q][:, two, :],
+                scalar=0.0,
+                in1=ph_of[(q, a)][:],
+                op0=ALU.max,
+                op1=ALU.mult,
             )
 
         def vector_tiles(q):
-            return UNITS[q] if q < NU - 4 else 0
+            return 0
 
         def relu_vector(q):
             lam = opool.tile([P, UNITS[q], D], F32)
@@ -239,30 +284,10 @@ def tile_gatel0rdcell_pa_t_kernel(tc, x_t, h_tminus1, gate_noise, Wg, bg, Wr, br
         def store_gate(q):
             nc.sync.dma_start(out=o1v[:, rows_of(q), :], in_=lam_of[q][:])
 
-        def gate(q):
-            d = d_of[q]
-            nc.vector.scalar_tensor_tensor(out=d[:], in0=t_of[q][:], scalar=0.0, in1=d[:], op0=ALU.max, op1=ALU.mult)
-
         def outputs(q):
             ht = opool.tile([P, UNITS[q], D], F32)
-            mine = UNITS[q] - 1 if q < NU - 3 and UNITS[q] == 4 else UNITS[q]
-            for i in range(mine, UNITS[q]):
-                nc.gpsimd.tensor_tensor(
-                    out=ht[:, i, :], in0=d_of[q][:, i, :], in1=g_of[q][:, i, D : 2 * D], op=ALU.add
-                )
-            nc.vector.tensor_tensor(
-                out=ht[:, 0:mine, :], in0=d_of[q][:, 0:mine, :], in1=g_of[q][:, 0:mine, D : 2 * D], op=ALU.add
-            )
+            nc.vector.tensor_tensor(out=ht[:], in0=e_of[q][:], in1=g_of[q][:, :, D : 2 * D], op=ALU.add)
             nc.sync.dma_start(out=o0v[:, rows_of(q), :], in_=ht[:])
-
-        b_col = const.tile([P, 4], F32)
-
-        def bias_columns():
-            b_f32 = const.tile([P, P], F32)
-            nc.vector.tensor_copy(out=b_f32[:], in_=b_rows[:])
-            b_ps = psum.tile([P, 2, D], F32, tag="ph")
-            nc.tensor.transpose(b_ps[:, 0, 0:P], b_f32[:], ident[:])
-            nc.vector.tensor_copy(out=b_col[:], in_=b_ps[:, 0, 0:4])
 
         def on(q):
             return 0 <= q < NU
@@ -271,83 +296,76 @@ def tile_gatel0rdcell_pa_t_kernel(tc, x_t, h_tminus1, gate_noise, Wg, bg, Wr, br
             return range(UNITS[q] // 2)
 
         def step(k):
-            q = k + 0
-            if on(q):
-                mx(q, 2)
-                mx(q, 3)
             q = k + 2
             if on(q):
                 g_transposes(q, 0)
+            q = k + 2
+            if on(q) and UNITS[q] == 4:
+                g_transposes(q, 1)
+            q = k + 2
+            if on(q):
+                g_evacuate(q, 0)
+            q = k + 2
+            if on(q) and UNITS[q] == 4:
+                g_evacuate(q, 1)
+            q = k - 1
+            if on(q):
+                relu_vector(q)
+            q = k + 1
+            if on(q):
+                for a in pairs(q):
+                    g_quantise(q, a)
             q = k - 1
             if on(q):
                 back_r(q, 0)
             q = k - 1
-            if on(q):
-                back_i(q, 0)
+            if on(q) and UNITS[q] == 4:
+                back_r(q, 1)
             q = k - 1
             if on(q):
-                subtract_noise(q, 0)
+                subtract_h(q, 0)
+            q = k - 1
+            if on(q) and UNITS[q] == 4:
+                subtract_h(q, 1)
+            q = k + 0
+            if on(q):
+                mx_r(q, 0)
+                mx_r(q, 1)
+            q = k + 0
+            if on(q):
+                mx_gate(q, 0)
+            q = k + 0
+            if on(q) and UNITS[q] == 4:
+                mx_gate(q, 1)
             q = k + 0
             if on(q):
                 tanh_r(q, 0)
             q = k + 0
             if on(q):
                 tanh_r(q, 1)
-            q = k + 2
+            q = k - 1
             if on(q):
-                g_evacuate(q, 0)
-            q = k + 1
-            if on(q):
-                for a in pairs(q):
-                    g_quantise(q, a)
-            q = k - 2
-            if on(q):
-                relu_vector(q)
-            q = k - 2
+                gate(q, 0)
+            q = k - 1
+            if on(q) and UNITS[q] == 4:
+                gate(q, 1)
+            q = k - 1
             if on(q):
                 relu_scalar(q)
                 store_gate(q)
-            q = k - 2
+            q = k + 1
             if on(q):
-                gate(q)
-            q = k - 1
-            if on(q):
-                diff(q, 0)
+                noise_bias(q)
             q = k + 0
             if on(q):
-                mx(q, 0)
-                mx(q, 1)
-            q = k + 2
+                add_i(q, 0)
+            q = k + 0
             if on(q) and UNITS[q] == 4:
-                g_transposes(q, 1)
-            q = k - 1
-            if on(q) and UNITS[q] == 4:
-                back_r(q, 1)
-            q = k - 1
-            if on(q) and UNITS[q] == 4:
-                back_i(q, 1)
-            q = k - 1
-            if on(q) and UNITS[q] == 4:
-                subtract_noise(q, 1)
+                add_i(q, 1)
             q = k + 0
             if on(q):
-                bias_i(q, 0)
-            q = k + 0
-            if on(q):
-                bias_i(q, 1)
+                tanh_i(q)
             q = k - 1
-            if on(q):
-                tanh_i(q, 0)
-            q = k + 2
-            if on(q) and UNITS[q] == 4:
-                g_evacuate(q, 1)
-            q = k - 1
-            if on(q) and UNITS[q] == 4:
-                tanh_i(q, 1)
-            q = k - 1
-            if on(q) and UNITS[q] == 4:
-                diff(q, 1)
-            q = k - 2
             if on(q):
                 outputs(q)
 
@@ -358,6 +376,6 @@ def tile_gatel0rdcell_pa_t_kernel(tc, x_t, h_tminus1, gate_noise, Wg, bg, Wr, br
                 if k >= 0 and on(k + LOOKAHEAD - 1):
                     load_n(k + LOOKAHEAD - 1)
                 step(k)
-                if k == -1:
-                    bias_columns()
+                if k == -2:
+                    biases()
                     weights(0)

@@ -36,6 +36,76 @@ def tile_gatel0rdcell_pa_t_kernel(tc, x_t, h_tminus1, gate_noise, Wg, bg, Wr, br
     o0v = out_0.rearrange("(p t) k -> p t k", t=NT)
     o1v = out_1.rearrange("(p t) k -> p t k", t=NT)
 
+    HEAD = (
+        ("L", 0),
+        ("WL", 1),
+        ("L", 1),
+        ("WL", 0),
+        ("N", 0),
+        ("L", 2),
+        ("N", 1),
+        ("L", 3),
+        ("N", 2),
+        ("L", 4),
+        ("N", 3),
+        ("Ng", 0),
+        ("Bb", 0),
+        ("g0", 0),
+        ("e0", 0),
+        ("g0", 1),
+        ("e0", 1),
+        ("W", 1),
+        ("q0", 0),
+        ("Bc", 0),
+        ("mra", 0),
+        ("mrb", 0),
+        ("Ra", 0),
+        ("Rb", 0),
+        ("W", 0),
+        ("q0", 1),
+        ("G", 0),
+        ("Gc", 0),
+        ("m0", 0),
+        ("n", 0),
+        ("g0", 2),
+        ("e0", 2),
+        ("g1", 2),
+        ("e1", 2),
+        ("n", 1),
+        ("u0", 0),
+        ("t0", 0),
+    )
+    ORDER = (
+        ("L", 5),
+        ("N", 4),
+        ("g0", 2),
+        ("g1", 2),
+        ("e0", 2),
+        ("e1", 2),
+        ("q0", 1),
+        ("q1", 1),
+        ("br0", -1),
+        ("br1", -1),
+        ("d0", -1),
+        ("d1", -1),
+        ("x0", -1),
+        ("x1", -1),
+        ("n", 1),
+        ("mra", 0),
+        ("mrb", 0),
+        ("m0", 0),
+        ("m1", 0),
+        ("Ra", 0),
+        ("Rb", 0),
+        ("rv", -1),
+        ("rs", -1),
+        ("u0", 0),
+        ("u1", 0),
+        ("t0", 0),
+        ("t1", 0),
+        ("o", -1),
+    )
+    AFTER = {}
     with ExitStack() as ctx:
         const = ctx.enter_context(tc.tile_pool(name="const", bufs=1))
         gpool = ctx.enter_context(tc.tile_pool(name="gpool", bufs=LOOKAHEAD + 5))
@@ -43,11 +113,10 @@ def tile_gatel0rdcell_pa_t_kernel(tc, x_t, h_tminus1, gate_noise, Wg, bg, Wr, br
         grpool = ctx.enter_context(tc.tile_pool(name="grpool", bufs=4))
         cpool = ctx.enter_context(tc.tile_pool(name="cpool", bufs=4))
         hpool = ctx.enter_context(tc.tile_pool(name="hpool", bufs=4))
-        nbpool = ctx.enter_context(tc.tile_pool(name="nbpool", bufs=2))
         upool = ctx.enter_context(tc.tile_pool(name="upool", bufs=3))
         tpool = ctx.enter_context(tc.tile_pool(name="tpool", bufs=3))
         dpool = ctx.enter_context(tc.tile_pool(name="dpool", bufs=3))
-        epool = ctx.enter_context(tc.tile_pool(name="epool", bufs=3))
+        nepool = ctx.enter_context(tc.tile_pool(name="nepool", bufs=3))
         opool = ctx.enter_context(tc.tile_pool(name="opool", bufs=4))
         psum = ctx.enter_context(tc.psum_pool(name="psum", bufs=2))
 
@@ -96,12 +165,6 @@ def tile_gatel0rdcell_pa_t_kernel(tc, x_t, h_tminus1, gate_noise, Wg, bg, Wr, br
         ident = const.tile([P, P], F32)
         make_identity(nc, ident[:])
         w_raw = const.tile([P, 2, 4, D], BF16)
-        load_g(0)
-        nc.sync.dma_start(out=w_raw[:, 1], in_=Wr.rearrange("(p j) w -> p j w", j=4))
-        nc.sync.dma_start(out=w_raw[:, 0], in_=Wg.rearrange("(p j) w -> p j w", j=4))
-        for q in range(1, LOOKAHEAD):
-            load_n(q - 1)
-            load_g(q)
 
         w_grp = const.tile([P, 2, D, 4], BF16, align_bytes=64)
         w_codes = const.tile([P, 2 * D], U32, align_bytes=64)
@@ -116,21 +179,38 @@ def tile_gatel0rdcell_pa_t_kernel(tc, x_t, h_tminus1, gate_noise, Wg, bg, Wr, br
                 in_=w_grp[:, m].rearrange("p w j -> p (w j)"),
             )
 
-        weights(1)
         neg_ident = const.tile([P, P], BF16)
-        nc.vector.tensor_scalar_mul(out=neg_ident[:], in0=ident[:], scalar1=-1.0)
+        b_f32 = const.tile([P, P], F32)
         br_col = const.tile([P, 2], F32)
         bg_b = const.tile([P, D], F32)
 
-        def biases():
-            bg_ps = psum.tile([P, 2, D], F32, tag="pu")
-            nc.tensor.matmul(out=bg_ps[:, 0, :], lhsT=ones[:], rhs=bg_row[:], start=True, stop=True)
-            nc.vector.tensor_copy(out=bg_b[:], in_=bg_ps[:, 0, :])
-            b_f32 = const.tile([P, P], F32)
-            nc.vector.tensor_copy(out=b_f32[:], in_=b_rows[:])
+        bias_of = {}
+
+        def bias_b():
+            nc.scalar.copy(out=b_f32[:], in_=b_rows[:])
             b_ps = psum.tile([P, 2, D], F32, tag="ph")
             nc.tensor.transpose(b_ps[:, 0, 0:P], b_f32[:], ident[:])
-            nc.vector.tensor_copy(out=br_col[:], in_=b_ps[:, 0, 0:2])
+            bias_of["r"] = b_ps
+
+        def bias_bc():
+            nc.vector.tensor_copy(out=br_col[:], in_=bias_of["r"][:, 0, 0:2])
+
+        def bias_g():
+            bg_ps = psum.tile([P, 2, D], F32, tag="pu")
+            nc.tensor.matmul(out=bg_ps[:, 0, :], lhsT=ones[:], rhs=bg_row[:], start=True, stop=True)
+            bias_of["g"] = bg_ps
+
+        def bias_gc(eng):
+            if eng:
+                nc.scalar.copy(out=bg_b[:], in_=bias_of["g"][:, 0, :])
+            else:
+                nc.vector.tensor_copy(out=bg_b[:], in_=bias_of["g"][:, 0, :])
+
+        def negate():
+            nc.scalar.mul(out=neg_ident[:], in_=ident[:], mul=-1.0)
+
+        def load_w(m):
+            nc.sync.dma_start(out=w_raw[:, m], in_=(Wg, Wr)[m].rearrange("(p j) w -> p j w", j=4))
 
         def g_transposes(q, a):
             gw = g_of[q][:].bitcast(F32).rearrange("p t (j e) -> p t e j", e=2)
@@ -196,7 +276,7 @@ def tile_gatel0rdcell_pa_t_kernel(tc, x_t, h_tminus1, gate_noise, Wg, bg, Wr, br
             hT_of[(q, f)] = hT
 
         def noise_bias(q):
-            nb = nbpool.tile([P, UNITS[q], D], F32)
+            nb = nepool.tile([P, UNITS[q], D], F32, tag="ne")
             for i in range(0, UNITS[q], 2):
                 n = 2
                 nc.gpsimd.tensor_tensor(
@@ -216,10 +296,12 @@ def tile_gatel0rdcell_pa_t_kernel(tc, x_t, h_tminus1, gate_noise, Wg, bg, Wr, br
                 out=u_of[q][:, two, :], in0=pu_of[(q, a)][:], in1=nb_of[q][:, two, :], op=ALU.subtract
             )
 
-        def tanh_i(q):
-            t = tpool.tile([P, UNITS[q], D], F32)
-            nc.scalar.activation(out=t[:], in_=u_of[q][:], func=ACT.Tanh)
-            t_of[q] = t
+        def tanh_i(q, a):
+            if a == 0:
+                t_new = tpool.tile([P, UNITS[q], D], F32)
+                t_of[q] = t_new
+            two = slice(2 * a, 2 * a + 2)
+            nc.scalar.activation(out=t_of[q][:, two, :], in_=u_of[q][:, two, :], func=ACT.Tanh)
 
         def back_r(q, a):
             alone = h_on_vector(FIRST[q] // 2 + a)
@@ -254,7 +336,7 @@ def tile_gatel0rdcell_pa_t_kernel(tc, x_t, h_tminus1, gate_noise, Wg, bg, Wr, br
 
         def gate(q, a):
             if a == 0:
-                e_new = epool.tile([P, UNITS[q], D], F32)
+                e_new = nepool.tile([P, UNITS[q], D], F32, tag="ne")
                 e_of[q] = e_new
             two = slice(2 * a, 2 * a + 2)
             nc.vector.scalar_tensor_tensor(
@@ -295,87 +377,44 @@ def tile_gatel0rdcell_pa_t_kernel(tc, x_t, h_tminus1, gate_noise, Wg, bg, Wr, br
         def pairs(q):
             return range(UNITS[q] // 2)
 
-        def step(k):
-            q = k + 2
-            if on(q):
-                g_transposes(q, 0)
-            q = k + 2
-            if on(q) and UNITS[q] == 4:
-                g_transposes(q, 1)
-            q = k + 2
-            if on(q):
-                g_evacuate(q, 0)
-            q = k + 2
-            if on(q) and UNITS[q] == 4:
-                g_evacuate(q, 1)
-            q = k - 1
-            if on(q):
-                relu_vector(q)
-            q = k + 1
-            if on(q):
-                for a in pairs(q):
-                    g_quantise(q, a)
-            q = k - 1
-            if on(q):
-                back_r(q, 0)
-            q = k - 1
-            if on(q) and UNITS[q] == 4:
-                back_r(q, 1)
-            q = k - 1
-            if on(q):
-                subtract_h(q, 0)
-            q = k - 1
-            if on(q) and UNITS[q] == 4:
-                subtract_h(q, 1)
-            q = k + 0
-            if on(q):
-                mx_r(q, 0)
-                mx_r(q, 1)
-            q = k + 0
-            if on(q):
-                mx_gate(q, 0)
-            q = k + 0
-            if on(q) and UNITS[q] == 4:
-                mx_gate(q, 1)
-            q = k + 0
-            if on(q):
-                tanh_r(q, 0)
-            q = k + 0
-            if on(q):
-                tanh_r(q, 1)
-            q = k - 1
-            if on(q):
-                gate(q, 0)
-            q = k - 1
-            if on(q) and UNITS[q] == 4:
-                gate(q, 1)
-            q = k - 1
-            if on(q):
-                relu_scalar(q)
-                store_gate(q)
-            q = k + 1
-            if on(q):
-                noise_bias(q)
-            q = k + 0
-            if on(q):
-                add_i(q, 0)
-            q = k + 0
-            if on(q) and UNITS[q] == 4:
-                add_i(q, 1)
-            q = k + 0
-            if on(q):
-                tanh_i(q)
-            q = k - 1
-            if on(q):
-                outputs(q)
+        done = set()
+
+        def skip(tok, q):
+            if (tok, q) in done or not on(q):
+                return True
+            done.add((tok, q))
+            return tok[-1] == "1" and tok[0] != "W" and UNITS[q] == 2
+
+        STAGES = {
+            "g0": lambda q: g_transposes(q, 0), "g1": lambda q: g_transposes(q, 1),
+            "e0": lambda q: g_evacuate(q, 0), "e1": lambda q: g_evacuate(q, 1),
+            "q0": lambda q: g_quantise(q, 0), "q1": lambda q: g_quantise(q, 1),
+            "mra": lambda q: mx_r(q, 0), "mrb": lambda q: mx_r(q, 1),
+            "m0": lambda q: mx_gate(q, 0), "m1": lambda q: mx_gate(q, 1),
+            "Ra": lambda q: tanh_r(q, 0), "Rb": lambda q: tanh_r(q, 1),
+            "br0": lambda q: back_r(q, 0), "br1": lambda q: back_r(q, 1),
+            "d0": lambda q: subtract_h(q, 0), "d1": lambda q: subtract_h(q, 1),
+            "x0": lambda q: gate(q, 0), "x1": lambda q: gate(q, 1),
+            "n": noise_bias,
+            "u0": lambda q: add_i(q, 0), "u1": lambda q: add_i(q, 1),
+            "t0": lambda q: tanh_i(q, 0), "t1": lambda q: tanh_i(q, 1),
+            "rv": relu_vector, "rs": lambda q: (relu_scalar(q), store_gate(q)), "o": outputs,
+            "L": load_g, "N": load_n,
+            "WL": load_w, "W": weights, "Bb": lambda q: bias_b(), "Bc": lambda q: bias_bc(), "G": lambda q: bias_g(), "Gc": bias_gc, "Ng": lambda q: negate(),
+        }
+
+        def do(calls):
+            for tok, q in calls:
+                if not skip(tok, q):
+                    STAGES[tok](q)
+
+        def step(k, order):
+            for tok, shift in order:
+                if not skip(tok, k + shift):
+                    STAGES[tok](k + shift)
 
         with tc.manual_schedule():
-            for k in range(-2, NU + 2):
-                if k >= 0 and on(k + LOOKAHEAD):
-                    load_g(k + LOOKAHEAD)
-                if k >= 0 and on(k + LOOKAHEAD - 1):
-                    load_n(k + LOOKAHEAD - 1)
-                step(k)
-                if k == -2:
-                    biases()
-                    weights(0)
+            do(HEAD)
+            for k in range(0, NU + 3):
+                step(k, ORDER)
+                do(AFTER.get(k, ()))

@@ -18,12 +18,18 @@ D = 256
 NT = 64
 UNITS = (2, 2, 4, 4, 4, 4, 4, 4, 4, 4, 4, 4, 4, 4, 4, 4, 2, 2)
 NU = 18
-LOOKAHEAD = 5
+VT = {}
+VTD = 0
+NBW = 4
+EV = ()
+ALONE = (3, 7, 11, 15, 19, 23, 27)
+GTL = {}
+LOOKAHEAD = 6
 GT_BANKS, PT_BANKS, PH_BANKS, PU_BANKS = 2, 2, 2, 2
 
 
 def h_on_vector(pair):
-    return pair % 4 == 1 and pair < 28
+    return pair in ALONE
 
 
 def tile_gatel0rdcell_pa_t_kernel(tc, x_t, h_tminus1, gate_noise, Wg, bg, Wr, br, out_0, out_1):
@@ -48,6 +54,8 @@ def tile_gatel0rdcell_pa_t_kernel(tc, x_t, h_tminus1, gate_noise, Wg, bg, Wr, br
         ("N", 2),
         ("L", 4),
         ("N", 3),
+        ("L", 5),
+        ("N", 4),
         ("Ng", 0),
         ("Bb", 0),
         ("g0", 0),
@@ -82,14 +90,15 @@ def tile_gatel0rdcell_pa_t_kernel(tc, x_t, h_tminus1, gate_noise, Wg, bg, Wr, br
         ("g1", 2),
         ("e0", 2),
         ("e1", 2),
-        ("q0", 1),
-        ("q1", 1),
         ("br0", -1),
         ("br1", -1),
-        ("d0", -1),
-        ("d1", -1),
-        ("x0", -1),
-        ("x1", -1),
+        ("xa", -2),
+        ("q0", 1),
+        ("q1", 1),
+        ("o0", -2),
+        ("o1", -2),
+        ("dd", -1),
+        ("xn", -1),
         ("n", 1),
         ("mra", 0),
         ("mrb", 0),
@@ -97,26 +106,27 @@ def tile_gatel0rdcell_pa_t_kernel(tc, x_t, h_tminus1, gate_noise, Wg, bg, Wr, br
         ("m1", 0),
         ("Ra", 0),
         ("Rb", 0),
-        ("rv", -1),
+        ("rn", -1),
         ("rs", -1),
+        ("sg", -1),
         ("u0", 0),
         ("u1", 0),
         ("t0", 0),
         ("t1", 0),
-        ("o", -1),
     )
     AFTER = {}
     with ExitStack() as ctx:
         const = ctx.enter_context(tc.tile_pool(name="const", bufs=1))
         gpool = ctx.enter_context(tc.tile_pool(name="gpool", bufs=LOOKAHEAD + 5))
         npool = ctx.enter_context(tc.tile_pool(name="npool", bufs=LOOKAHEAD + 2))
-        grpool = ctx.enter_context(tc.tile_pool(name="grpool", bufs=4))
-        cpool = ctx.enter_context(tc.tile_pool(name="cpool", bufs=4))
+        grpool = ctx.enter_context(tc.tile_pool(name="grpool", bufs=6))
+        cpool = ctx.enter_context(tc.tile_pool(name="cpool", bufs=5))
         hpool = ctx.enter_context(tc.tile_pool(name="hpool", bufs=4))
         upool = ctx.enter_context(tc.tile_pool(name="upool", bufs=3))
         tpool = ctx.enter_context(tc.tile_pool(name="tpool", bufs=3))
         dpool = ctx.enter_context(tc.tile_pool(name="dpool", bufs=3))
         nepool = ctx.enter_context(tc.tile_pool(name="nepool", bufs=3))
+        e1pool = ctx.enter_context(tc.tile_pool(name="e1pool", bufs=3))
         opool = ctx.enter_context(tc.tile_pool(name="opool", bufs=4))
         psum = ctx.enter_context(tc.psum_pool(name="psum", bufs=2))
 
@@ -135,6 +145,7 @@ def tile_gatel0rdcell_pa_t_kernel(tc, x_t, h_tminus1, gate_noise, Wg, bg, Wr, br
         t_of = {}
         e_of = {}
         lam_of = {}
+        ht_of = {}
 
         def rows_of(q):
             return slice(FIRST[q], FIRST[q] + UNITS[q])
@@ -277,8 +288,8 @@ def tile_gatel0rdcell_pa_t_kernel(tc, x_t, h_tminus1, gate_noise, Wg, bg, Wr, br
 
         def noise_bias(q):
             nb = nepool.tile([P, UNITS[q], D], F32, tag="ne")
-            for i in range(0, UNITS[q], 2):
-                n = 2
+            for i in range(0, UNITS[q], NBW):
+                n = min(NBW, UNITS[q])
                 nc.gpsimd.tensor_tensor(
                     out=nb[:, i : i + n, :],
                     in0=nz_of[q][:, i : i + n, :],
@@ -334,42 +345,50 @@ def tile_gatel0rdcell_pa_t_kernel(tc, x_t, h_tminus1, gate_noise, Wg, bg, Wr, br
                 )
                 ph_of[(q, a)] = d
 
+        def tanh_whole(q):
+            t_new = tpool.tile([P, UNITS[q], D], F32)
+            t_of[q] = t_new
+            nc.scalar.activation(out=t_new[:], in_=u_of[q][:], func=ACT.Tanh)
+
         def gate(q, a):
-            if a == 0:
-                e_new = nepool.tile([P, UNITS[q], D], F32, tag="ne")
-                e_of[q] = e_new
-            two = slice(2 * a, 2 * a + 2)
+            pool = (nepool, e1pool)[a]
+            e_new = pool.tile([P, 2, D], F32, tag=("ne", "e1")[a])
+            e_of[(q, a)] = e_new
             nc.vector.scalar_tensor_tensor(
-                out=e_of[q][:, two, :],
-                in0=t_of[q][:, two, :],
+                out=e_new[:],
+                in0=t_of[q][:, 2 * a : 2 * a + 2, :],
                 scalar=0.0,
                 in1=ph_of[(q, a)][:],
                 op0=ALU.max,
                 op1=ALU.mult,
             )
 
-        def vector_tiles(q):
-            return 0
-
-        def relu_vector(q):
+        def relu_new(q):
             lam = opool.tile([P, UNITS[q], D], F32)
             lam_of[q] = lam
-            share = vector_tiles(q)
-            if share > 0:
-                nc.vector.tensor_scalar_max(out=lam[:, 0:share, :], in0=t_of[q][:, 0:share, :], scalar1=0.0)
 
-        def relu_scalar(q):
-            share = vector_tiles(q)
-            if UNITS[q] > share:
-                nc.scalar.activation(out=lam_of[q][:, share:, :], in_=t_of[q][:, share:, :], func=ACT.Relu)
+        def relu_part(q, eng):
+            v, g = VT.get(q, VTD if UNITS[q] == 4 else 0), GTL.get(q, 0)
+            if eng == "V" and v:
+                nc.vector.tensor_scalar_max(out=lam_of[q][:, 0:v, :], in0=t_of[q][:, 0:v, :], scalar1=0.0)
+            if eng == "G" and g:
+                nc.gpsimd.tensor_scalar(out=lam_of[q][:, v:v + g, :], in0=t_of[q][:, v:v + g, :], scalar1=0.0, scalar2=1.0, op0=ALU.max, op1=ALU.mult)
+            if eng == "S" and v + g < UNITS[q]:
+                nc.scalar.activation(out=lam_of[q][:, v + g:, :], in_=t_of[q][:, v + g:, :], func=ACT.Relu)
 
         def store_gate(q):
             nc.sync.dma_start(out=o1v[:, rows_of(q), :], in_=lam_of[q][:])
 
-        def outputs(q):
-            ht = opool.tile([P, UNITS[q], D], F32)
-            nc.vector.tensor_tensor(out=ht[:], in0=e_of[q][:], in1=g_of[q][:, :, D : 2 * D], op=ALU.add)
-            nc.sync.dma_start(out=o0v[:, rows_of(q), :], in_=ht[:])
+        def outputs(q, a):
+            if a == 0:
+                ht_new = opool.tile([P, UNITS[q], D], F32)
+                ht_of[q] = ht_new
+            two = slice(2 * a, 2 * a + 2)
+            nc.vector.tensor_tensor(
+                out=ht_of[q][:, two, :], in0=e_of[(q, a)][:], in1=g_of[q][:, two, D : 2 * D], op=ALU.add
+            )
+            if 2 * a + 2 == UNITS[q]:
+                nc.sync.dma_start(out=o0v[:, rows_of(q), :], in_=ht_of[q][:])
 
         def on(q):
             return 0 <= q < NU
@@ -398,7 +417,11 @@ def tile_gatel0rdcell_pa_t_kernel(tc, x_t, h_tminus1, gate_noise, Wg, bg, Wr, br
             "n": noise_bias,
             "u0": lambda q: add_i(q, 0), "u1": lambda q: add_i(q, 1),
             "t0": lambda q: tanh_i(q, 0), "t1": lambda q: tanh_i(q, 1),
-            "rv": relu_vector, "rs": lambda q: (relu_scalar(q), store_gate(q)), "o": outputs,
+            "rn": relu_new, "rv": lambda q: relu_part(q, "V"), "rg": lambda q: relu_part(q, "G"), "rs": lambda q: relu_part(q, "S"), "sg": store_gate, "o0": lambda q: outputs(q, 0), "o1": lambda q: outputs(q, 1),
+            "dd": lambda q: [subtract_h(q, a) for a in pairs(q)],
+            "xn": lambda q: [gate(q, a) for a in pairs(q) if not h_on_vector(FIRST[q] // 2 + a)],
+            "xa": lambda q: [gate(q, a) for a in pairs(q) if h_on_vector(FIRST[q] // 2 + a)],
+            "tt": lambda q: tanh_whole(q),
             "L": load_g, "N": load_n,
             "WL": load_w, "W": weights, "Bb": lambda q: bias_b(), "Bc": lambda q: bias_bc(), "G": lambda q: bias_g(), "Gc": bias_gc, "Ng": lambda q: negate(),
         }

@@ -21,8 +21,10 @@ NU = 18
 VT = {}
 VTD = 0
 NBW = 4
+PAIRED = 14
+OG = ()
 EV = ()
-ALONE = (3, 7, 11, 15, 19, 23, 27)
+ALONE = (3, 7, 11, 15, 19, 23, 31)
 GTL = {}
 LOOKAHEAD = 6
 GT_BANKS, PT_BANKS, PH_BANKS, PU_BANKS = 2, 2, 2, 2
@@ -118,7 +120,7 @@ def tile_gatel0rdcell_pa_t_kernel(tc, x_t, h_tminus1, gate_noise, Wg, bg, Wr, br
     with ExitStack() as ctx:
         const = ctx.enter_context(tc.tile_pool(name="const", bufs=1))
         gpool = ctx.enter_context(tc.tile_pool(name="gpool", bufs=LOOKAHEAD + 5))
-        npool = ctx.enter_context(tc.tile_pool(name="npool", bufs=LOOKAHEAD + 2))
+        npool = ctx.enter_context(tc.tile_pool(name="npool", bufs=4))
         grpool = ctx.enter_context(tc.tile_pool(name="grpool", bufs=6))
         cpool = ctx.enter_context(tc.tile_pool(name="cpool", bufs=5))
         hpool = ctx.enter_context(tc.tile_pool(name="hpool", bufs=4))
@@ -127,7 +129,7 @@ def tile_gatel0rdcell_pa_t_kernel(tc, x_t, h_tminus1, gate_noise, Wg, bg, Wr, br
         dpool = ctx.enter_context(tc.tile_pool(name="dpool", bufs=3))
         nepool = ctx.enter_context(tc.tile_pool(name="nepool", bufs=3))
         e1pool = ctx.enter_context(tc.tile_pool(name="e1pool", bufs=3))
-        opool = ctx.enter_context(tc.tile_pool(name="opool", bufs=4))
+        opool = ctx.enter_context(tc.tile_pool(name="opool", bufs=3))
         psum = ctx.enter_context(tc.psum_pool(name="psum", bufs=2))
 
         g_of = {}
@@ -146,6 +148,8 @@ def tile_gatel0rdcell_pa_t_kernel(tc, x_t, h_tminus1, gate_noise, Wg, bg, Wr, br
         e_of = {}
         lam_of = {}
         ht_of = {}
+        lams = {}
+        hts = {}
 
         def rows_of(q):
             return slice(FIRST[q], FIRST[q] + UNITS[q])
@@ -157,9 +161,13 @@ def tile_gatel0rdcell_pa_t_kernel(tc, x_t, h_tminus1, gate_noise, Wg, bg, Wr, br
             g_of[q] = g
 
         def load_n(q):
-            nz = npool.tile([P, UNITS[q], D], BF16)
-            nc.sync.dma_start(out=nz[:], in_=nv[:, rows_of(q), :])
-            nz_of[q] = nz
+            if q % 2:
+                return
+            lo, hi = FIRST[q], FIRST[q] + UNITS[q] + UNITS[q + 1]
+            nz = npool.tile([P, hi - lo, D], BF16)
+            nc.sync.dma_start(out=nz[:], in_=nv[:, lo:hi, :])
+            nz_of[q] = nz[:, 0 : UNITS[q], :]
+            nz_of[q + 1] = nz[:, UNITS[q] : hi - lo, :]
 
         b_rows = const.tile([P, P], BF16)
         nc.vector.memset(b_rows[:], 0.0)
@@ -363,9 +371,27 @@ def tile_gatel0rdcell_pa_t_kernel(tc, x_t, h_tminus1, gate_noise, Wg, bg, Wr, br
                 op1=ALU.mult,
             )
 
+        def store_group(q):
+            if q < PAIRED:
+                return q - q % 2, q - q % 2 + 1
+            return q, q
+
+        def out_tile(q, tiles, name):
+            first, last = store_group(q)
+            if q == first:
+                new = opool.tile([P, FIRST[last] + UNITS[last] - FIRST[first], D], F32, name=name)
+                tiles[first] = new
+            lo = FIRST[q] - FIRST[first]
+            tiles[q, 0] = tiles[first][:, lo : lo + UNITS[q], :]
+
+        def store(q, tiles, view):
+            first, last = store_group(q)
+            if q == last:
+                nc.sync.dma_start(out=view[:, FIRST[first] : FIRST[last] + UNITS[last], :], in_=tiles[first][:])
+
         def relu_new(q):
-            lam = opool.tile([P, UNITS[q], D], F32)
-            lam_of[q] = lam
+            out_tile(q, lams, "lam")
+            lam_of[q] = lams[q, 0]
 
         def relu_part(q, eng):
             v, g = VT.get(q, VTD if UNITS[q] == 4 else 0), GTL.get(q, 0)
@@ -377,18 +403,18 @@ def tile_gatel0rdcell_pa_t_kernel(tc, x_t, h_tminus1, gate_noise, Wg, bg, Wr, br
                 nc.scalar.activation(out=lam_of[q][:, v + g:, :], in_=t_of[q][:, v + g:, :], func=ACT.Relu)
 
         def store_gate(q):
-            nc.sync.dma_start(out=o1v[:, rows_of(q), :], in_=lam_of[q][:])
+            store(q, lams, o1v)
 
         def outputs(q, a):
             if a == 0:
-                ht_new = opool.tile([P, UNITS[q], D], F32)
-                ht_of[q] = ht_new
+                out_tile(q, hts, "ht")
+                ht_of[q] = hts[q, 0]
             two = slice(2 * a, 2 * a + 2)
-            nc.vector.tensor_tensor(
+            (nc.gpsimd if q in OG else nc.vector).tensor_tensor(
                 out=ht_of[q][:, two, :], in0=e_of[(q, a)][:], in1=g_of[q][:, two, D : 2 * D], op=ALU.add
             )
             if 2 * a + 2 == UNITS[q]:
-                nc.sync.dma_start(out=o0v[:, rows_of(q), :], in_=ht_of[q][:])
+                store(q, hts, o0v)
 
         def on(q):
             return 0 <= q < NU

@@ -16,16 +16,16 @@ ACT = mybir.ActivationFunctionType
 P = 128
 D = 256
 NT = 64
+NPAIRS = NT // 2
 UNITS = (2, 2, 4, 4, 4, 4, 4, 4, 4, 4, 4, 4, 4, 4, 4, 4, 2, 2)
 NU = 18
 VT = {}
 VTD = 0
 NBW = 4
-PAIRED = 14
-OG = ()
-EV = ()
-ALONE = (3, 7, 11, 15, 19, 23, 31)
+PAIRED = 10
+ALONE = (3, 7, 11, 15, 19, 23, 27)
 GTL = {}
+PLAIN = 4
 LOOKAHEAD = 6
 GT_BANKS, PT_BANKS, PH_BANKS, PU_BANKS = 2, 2, 2, 2
 
@@ -38,8 +38,8 @@ def tile_gatel0rdcell_pa_t_kernel(tc, x_t, h_tminus1, gate_noise, Wg, bg, Wr, br
     nc = tc.nc
     assert len(UNITS) == NU and sum(UNITS) == NT
     FIRST = [sum(UNITS[:u]) for u in range(NU)]
-    xv = x_t.rearrange("(p t) k -> p t k", t=NT)
-    hv = h_tminus1.rearrange("(p t) k -> p t k", t=NT)
+    xf = x_t.rearrange("(p t) k -> p (t k)", t=NT)
+    hf = h_tminus1.rearrange("(p t) k -> p (t k)", t=NT)
     nv = gate_noise.rearrange("(p t) k -> p t k", t=NT)
     o0v = out_0.rearrange("(p t) k -> p t k", t=NT)
     o1v = out_1.rearrange("(p t) k -> p t k", t=NT)
@@ -64,15 +64,19 @@ def tile_gatel0rdcell_pa_t_kernel(tc, x_t, h_tminus1, gate_noise, Wg, bg, Wr, br
         ("e0", 0),
         ("g0", 1),
         ("e0", 1),
-        ("W", 1),
-        ("q0", 0),
+        ("Wc", 1),
+        ("SW", 1),
+        ("W", 3),
+        ("q", 0),
         ("Bc", 0),
         ("mra", 0),
         ("mrb", 0),
         ("Ra", 0),
         ("Rb", 0),
-        ("W", 0),
-        ("q0", 1),
+        ("Wc", 0),
+        ("SW", 0),
+        ("W", 2),
+        ("q", 1),
         ("G", 0),
         ("Gc", 0),
         ("m0", 0),
@@ -94,18 +98,17 @@ def tile_gatel0rdcell_pa_t_kernel(tc, x_t, h_tminus1, gate_noise, Wg, bg, Wr, br
         ("e1", 2),
         ("br0", -1),
         ("br1", -1),
-        ("xa", -2),
-        ("q0", 1),
-        ("q1", 1),
+        ("q", 1),
         ("o0", -2),
         ("o1", -2),
-        ("dd", -1),
-        ("xn", -1),
+        ("x0", -1),
+        ("x1", -1),
         ("n", 1),
         ("mra", 0),
         ("mrb", 0),
         ("m0", 0),
         ("m1", 0),
+        ("hx", 0),
         ("Ra", 0),
         ("Rb", 0),
         ("rn", -1),
@@ -113,15 +116,18 @@ def tile_gatel0rdcell_pa_t_kernel(tc, x_t, h_tminus1, gate_noise, Wg, bg, Wr, br
         ("sg", -1),
         ("u0", 0),
         ("u1", 0),
+        ("hn", 0),
         ("t0", 0),
         ("t1", 0),
     )
-    AFTER = {}
+    AFTER = {2: (
+        ("W", 1),
+        ("W", 0),
+    )}
     with ExitStack() as ctx:
         const = ctx.enter_context(tc.tile_pool(name="const", bufs=1))
-        gpool = ctx.enter_context(tc.tile_pool(name="gpool", bufs=LOOKAHEAD + 5))
         npool = ctx.enter_context(tc.tile_pool(name="npool", bufs=4))
-        grpool = ctx.enter_context(tc.tile_pool(name="grpool", bufs=6))
+        grpool = ctx.enter_context(tc.tile_pool(name="grpool", bufs=3))
         cpool = ctx.enter_context(tc.tile_pool(name="cpool", bufs=5))
         hpool = ctx.enter_context(tc.tile_pool(name="hpool", bufs=4))
         upool = ctx.enter_context(tc.tile_pool(name="upool", bufs=3))
@@ -132,7 +138,6 @@ def tile_gatel0rdcell_pa_t_kernel(tc, x_t, h_tminus1, gate_noise, Wg, bg, Wr, br
         opool = ctx.enter_context(tc.tile_pool(name="opool", bufs=3))
         psum = ctx.enter_context(tc.psum_pool(name="psum", bufs=2))
 
-        g_of = {}
         nz_of = {}
         gt_of = {}
         gr_of = {}
@@ -150,15 +155,48 @@ def tile_gatel0rdcell_pa_t_kernel(tc, x_t, h_tminus1, gate_noise, Wg, bg, Wr, br
         ht_of = {}
         lams = {}
         hts = {}
+        hp_of = {}
+        nh_of = {}
 
         def rows_of(q):
             return slice(FIRST[q], FIRST[q] + UNITS[q])
 
+        gall = const.tile([P, NPAIRS * 4 * D], BF16)
+        g_pairs = gall[:].rearrange("p (n c) -> p n c", c=4 * D)
+        g_slots = gall[:].rearrange("p (n s d) -> p n s d", s=4, d=D)
+        g_words = gall[:].bitcast(F32)
+
+        def pairs_of(q):
+            return FIRST[q] // 2, (FIRST[q] + UNITS[q]) // 2
+
         def load_g(q):
-            g = gpool.tile([P, UNITS[q], 2 * D], BF16)
-            nc.sync.dma_start(out=g[:, :, 0:D], in_=xv[:, rows_of(q), :])
-            nc.sync.dma_start(out=g[:, :, D : 2 * D], in_=hv[:, rows_of(q), :])
-            g_of[q] = g
+            a, b = pairs_of(q)
+            if q < PLAIN:
+                nc.sync.dma_start(out=g_slots[:, a:b, 0::2, :].rearrange("p n s d -> p (n s) d"), in_=xf[:, a * 2 * D : b * 2 * D].rearrange("p (t d) -> p t d", d=D))
+                nc.sync.dma_start(out=g_slots[:, a:b, 1::2, :].rearrange("p n s d -> p (n s) d"), in_=hf[:, a * 2 * D : b * 2 * D].rearrange("p (t d) -> p t d", d=D))
+                return
+            if q == PLAIN:
+                nc.sync.dma_start(out=gall[:, 4 * a * D : (4 * a + 1) * D], in_=hf[:, 2 * a * D : (2 * a + 1) * D])
+            nc.sync.dma_start(
+                out=g_pairs[:, a:b, D : 3 * D],
+                in_=xf[:, a * 2 * D : b * 2 * D].rearrange("p (n c) -> p n c", c=2 * D),
+            )
+            last = b == NPAIRS
+            if last:
+                b = b - 1
+            if b > a:
+                nc.sync.dma_start(
+                    out=gall[:, (4 * a + 3) * D : (4 * b + 3) * D].rearrange("p (n c) -> p n c", c=4 * D)[:, :, 0 : 2 * D],
+                    in_=hf[:, (2 * a + 1) * D : (2 * b + 1) * D].rearrange("p (n c) -> p n c", c=2 * D),
+                )
+            if last:
+                nc.sync.dma_start(out=gall[:, (4 * b + 3) * D : (4 * b + 4) * D], in_=hf[:, (2 * b + 1) * D : (2 * b + 2) * D])
+
+        def h_rows(q, n0, n1):
+            a, b = pairs_of(q)
+            if q < PLAIN:
+                return g_slots[:, a + n0 : a + n1, 1::2, :]
+            return g_slots[:, a + n0 : a + n1, 0::3, :]
 
         def load_n(q):
             if q % 2:
@@ -184,24 +222,44 @@ def tile_gatel0rdcell_pa_t_kernel(tc, x_t, h_tminus1, gate_noise, Wg, bg, Wr, br
         ident = const.tile([P, P], F32)
         make_identity(nc, ident[:])
         w_raw = const.tile([P, 2, 4, D], BF16)
+        H = P // 2
 
-        w_grp = const.tile([P, 2, D, 4], BF16, align_bytes=64)
-        w_codes = const.tile([P, 2 * D], U32, align_bytes=64)
-        w_scales = const.tile([P, 2 * D], U8, align_bytes=64)
+        def load_w(m):
+            nc.sync.dma_start(out=w_raw[:, m], in_=(Wg, Wr)[m].rearrange("(p j) w -> p j w", j=4))
 
-        def weights(m):
-            nc.vector.tensor_copy(out=w_grp[:, m], in_=w_raw[:, m].rearrange("p j w -> p w j"))
-            cols = slice(m * D, (m + 1) * D)
+        w_grp = const.tile([P, 2, 2, D, 4], BF16, align_bytes=64)
+        w_codes = const.tile([P, 4 * D], U32, align_bytes=64)
+        w_scales = const.tile([P, 4 * D], U8, align_bytes=64)
+
+        def w_cols(side, m, lo, hi):
+            return slice((2 * side + m) * D + lo, (2 * side + m) * D + hi)
+
+        def weights_group(m):
+            nc.vector.tensor_copy(out=w_grp[:, 1, m], in_=w_raw[:, m].rearrange("p j w -> p w j"))
+
+        def swap(m):
+            nc.sync.dma_start(out=w_grp[0:H, 0, m], in_=w_grp[H:P, 1, m])
+            nc.sync.dma_start(out=w_grp[H:P, 0, m], in_=w_grp[0:H, 1, m])
+
+        def copy_on(eng, out, in_):
+            if eng:
+                nc.scalar.copy(out=out, in_=in_)
+            else:
+                nc.vector.tensor_copy(out=out, in_=in_)
+
+        def weights(side, m):
+            cols = w_cols(side, m, 0, D)
             nc.vector.quantize_mx(
                 out=w_codes[:, cols].bitcast(FP8X4),
                 scales=w_scales[:, cols],
-                in_=w_grp[:, m].rearrange("p w j -> p (w j)"),
+                in_=w_grp[:, side, m].rearrange("p w j -> p (w j)"),
             )
 
         neg_ident = const.tile([P, P], BF16)
+        ident_b = const.tile([P, P], BF16)
         b_f32 = const.tile([P, P], F32)
         br_col = const.tile([P, 2], F32)
-        bg_b = const.tile([P, D], F32)
+        bg_b = const.tile([P, D], BF16)
 
         bias_of = {}
 
@@ -227,61 +285,65 @@ def tile_gatel0rdcell_pa_t_kernel(tc, x_t, h_tminus1, gate_noise, Wg, bg, Wr, br
 
         def negate():
             nc.scalar.mul(out=neg_ident[:], in_=ident[:], mul=-1.0)
-
-        def load_w(m):
-            nc.sync.dma_start(out=w_raw[:, m], in_=(Wg, Wr)[m].rearrange("(p j) w -> p j w", j=4))
+            nc.scalar.copy(out=ident_b[:], in_=ident[:])
 
         def g_transposes(q, a):
-            gw = g_of[q][:].bitcast(F32).rearrange("p t (j e) -> p t e j", e=2)
             gt = psum.tile([P, 2, 2, P], F32, tag="gt", bufs=GT_BANKS)
+            n = UNITS[q] // 2
             for i in range(2):
+                pair, side = (2 * a + i) % n, (2 * a + i) // n
+                w0 = (4 * (FIRST[q] // 2 + pair) + 2 * side) * (D // 2)
                 for e in range(2):
-                    nc.tensor.transpose(gt[:, e, i, :], gw[:, 2 * a + i, e, :], ident[:])
+                    nc.tensor.transpose(gt[:, e, i, :], g_words[:, w0 + e : w0 + D : 2], ident[:])
             gt_of[(q, a)] = gt
 
         def g_evacuate(q, a):
-            gr = grpool.tile([P, 4 * 2 * P], BF16, align_bytes=64)
+            if a == 0:
+                gr_new = grpool.tile([P, UNITS[q] * 4 * P], BF16, align_bytes=64)
+                gr_of[q] = gr_new
             nc.scalar.copy(
-                out=gr[:].bitcast(F32).rearrange("p (c e) -> p c e", e=2),
+                out=gr_of[q][:, a * 8 * P : (a + 1) * 8 * P].bitcast(F32).rearrange("p (c e) -> p c e", e=2),
                 in_=gt_of[(q, a)][:].rearrange("p e i l -> p (i l) e"),
             )
-            gr_of[(q, a)] = gr
 
-        def g_quantise(q, a):
-            if a == 0:
-                gc_new = cpool.tile([P, UNITS[q] * P], U32, align_bytes=64)
-                gs_new = cpool.tile([P, UNITS[q] * P], U8, align_bytes=64)
-                gc_of[q] = gc_new
-                gs_of[q] = gs_new
-            cols = slice(a * 2 * P, (a + 1) * 2 * P)
-            nc.vector.quantize_mx(
-                out=gc_of[q][:, cols].bitcast(FP8X4), scales=gs_of[q][:, cols], in_=gr_of[(q, a)][:]
-            )
+        def g_quantise(q):
+            gc = cpool.tile([P, UNITS[q] * P], U32, align_bytes=64)
+            gs = cpool.tile([P, UNITS[q] * P], U8, align_bytes=64)
+            nc.vector.quantize_mx(out=gc[:].bitcast(FP8X4), scales=gs[:], in_=gr_of[q][:])
+            gc_of[q] = gc
+            gs_of[q] = gs
 
         def mx_r(q, f):
             pt = psum.tile([P, UNITS[q] * P], F32, tag="pt", bufs=PT_BANKS)
-            wcols = slice(D + f * P, D + (f + 1) * P)
-            nc.tensor.matmul_mx(
-                out=pt[:],
-                lhsT=w_codes[:, wcols].bitcast(FP8X4),
-                lhsT_scale=w_scales[:, wcols],
-                rhs=gc_of[q][:].bitcast(FP8X4),
-                rhs_scale=gs_of[q][:],
-                start=True,
-                stop=True,
-            )
+            half = UNITS[q] // 2 * P
+            for side in range(2):
+                if q < PLAIN and side == 1:
+                    continue
+                wcols = w_cols(1 if q < PLAIN else side, 1, f * P, (f + 1) * P)
+                cols = slice(0, 2 * half) if q < PLAIN else slice(side * half, (side + 1) * half)
+                nc.tensor.matmul_mx(
+                    out=pt[:, cols],
+                    lhsT=w_codes[:, wcols].bitcast(FP8X4),
+                    lhsT_scale=w_scales[:, wcols],
+                    rhs=gc_of[q][:, cols].bitcast(FP8X4),
+                    rhs_scale=gs_of[q][:, cols],
+                    start=True,
+                    stop=True,
+                )
             pt_of[(q, f)] = pt
 
         def mx_gate(q, a):
             pu = psum.tile([P, 2, D], F32, tag="pu", bufs=PU_BANKS)
             for i in range(2):
-                cols = slice((2 * a + i) * P, (2 * a + i + 1) * P)
+                c = i * (UNITS[q] // 2) + a
+                cols = slice(c * P, (c + 1) * P)
+                wcols = w_cols(1 if q < PLAIN else i, 0, 0, D)
                 nc.tensor.matmul_mx(
                     out=pu[:, i, :],
                     lhsT=gc_of[q][:, cols].bitcast(FP8X4),
                     lhsT_scale=gs_of[q][:, cols],
-                    rhs=w_codes[:, 0:D].bitcast(FP8X4),
-                    rhs_scale=w_scales[:, 0:D],
+                    rhs=w_codes[:, wcols].bitcast(FP8X4),
+                    rhs_scale=w_scales[:, wcols],
                     start=True,
                     stop=True,
                 )
@@ -322,41 +384,42 @@ def tile_gatel0rdcell_pa_t_kernel(tc, x_t, h_tminus1, gate_noise, Wg, bg, Wr, br
             two = slice(2 * a, 2 * a + 2)
             nc.scalar.activation(out=t_of[q][:, two, :], in_=u_of[q][:, two, :], func=ACT.Tanh)
 
+        def turn_h(q, a):
+            if h_on_vector(FIRST[q] // 2 + a):
+                hp = psum.tile([P, 2, 2, P], BF16, tag="ph", bufs=PH_BANKS)
+                for i in range(2):
+                    for f in range(2):
+                        nc.tensor.transpose(hp[:, i, f, :], h_rows(q, a, a + 1)[:, 0, i, f * P : (f + 1) * P], ident_b[:])
+                hp_of[q, a] = hp
+
+        def negate_h(q, a):
+            if h_on_vector(FIRST[q] // 2 + a):
+                nh = dpool.tile([P, 2, 2, P], F32)
+                nc.vector.tensor_scalar_mul(out=nh[:], in0=hp_of[q, a][:], scalar1=-1.0)
+                nh_of[q, a] = nh
+
         def back_r(q, a):
             alone = h_on_vector(FIRST[q] // 2 + a)
             ph = psum.tile([P, 2, D], F32, tag="ph", bufs=PH_BANKS)
             if not alone:
-                nc.tensor.matmul(
-                    out=ph[:],
-                    lhsT=neg_ident[:],
-                    rhs=g_of[q][:, 2 * a : 2 * a + 2, D : 2 * D],
-                    start=True,
-                    stop=False,
-                )
+                nc.tensor.matmul(out=ph[:], lhsT=neg_ident[:], rhs=h_rows(q, a, a + 1)[:, 0], start=True, stop=False)
             for i in range(2):
+                c = (i * (UNITS[q] // 2) + a)
                 for f in range(2):
+                    region = ph[:, i, f * P : (f + 1) * P]
                     nc.tensor.matmul(
-                        out=ph[:, i, f * P : (f + 1) * P],
-                        lhsT=hT_of[(q, f)][:, (2 * a + i) * P : (2 * a + i + 1) * P],
+                        out=region,
+                        lhsT=hT_of[(q, f)][:, c * P : (c + 1) * P],
                         rhs=ident[:],
                         is_transpose=True,
                         start=alone,
-                        stop=(i == 1 and f == 1) or alone,
+                        stop=not alone and i == 1 and f == 1,
                     )
+                    if alone:
+                        nc.tensor.matmul(
+                            out=region, lhsT=nh_of[q, a][:, i, f, :], rhs=ident[:], is_transpose=True, start=False, stop=True
+                        )
             ph_of[(q, a)] = ph
-
-        def subtract_h(q, a):
-            if h_on_vector(FIRST[q] // 2 + a):
-                d = dpool.tile([P, 2, D], F32)
-                nc.vector.tensor_tensor(
-                    out=d[:], in0=ph_of[(q, a)][:], in1=g_of[q][:, 2 * a : 2 * a + 2, D : 2 * D], op=ALU.subtract
-                )
-                ph_of[(q, a)] = d
-
-        def tanh_whole(q):
-            t_new = tpool.tile([P, UNITS[q], D], F32)
-            t_of[q] = t_new
-            nc.scalar.activation(out=t_new[:], in_=u_of[q][:], func=ACT.Tanh)
 
         def gate(q, a):
             pool = (nepool, e1pool)[a]
@@ -410,8 +473,8 @@ def tile_gatel0rdcell_pa_t_kernel(tc, x_t, h_tminus1, gate_noise, Wg, bg, Wr, br
                 out_tile(q, hts, "ht")
                 ht_of[q] = hts[q, 0]
             two = slice(2 * a, 2 * a + 2)
-            (nc.gpsimd if q in OG else nc.vector).tensor_tensor(
-                out=ht_of[q][:, two, :], in0=e_of[(q, a)][:], in1=g_of[q][:, two, D : 2 * D], op=ALU.add
+            nc.vector.tensor_tensor(
+                out=ht_of[q][:, two, :], in0=e_of[(q, a)][:], in1=h_rows(q, a, a + 1)[:, 0], op=ALU.add
             )
             if 2 * a + 2 == UNITS[q]:
                 store(q, hts, o0v)
@@ -433,23 +496,19 @@ def tile_gatel0rdcell_pa_t_kernel(tc, x_t, h_tminus1, gate_noise, Wg, bg, Wr, br
         STAGES = {
             "g0": lambda q: g_transposes(q, 0), "g1": lambda q: g_transposes(q, 1),
             "e0": lambda q: g_evacuate(q, 0), "e1": lambda q: g_evacuate(q, 1),
-            "q0": lambda q: g_quantise(q, 0), "q1": lambda q: g_quantise(q, 1),
+            "q": g_quantise,
             "mra": lambda q: mx_r(q, 0), "mrb": lambda q: mx_r(q, 1),
             "m0": lambda q: mx_gate(q, 0), "m1": lambda q: mx_gate(q, 1),
             "Ra": lambda q: tanh_r(q, 0), "Rb": lambda q: tanh_r(q, 1),
             "br0": lambda q: back_r(q, 0), "br1": lambda q: back_r(q, 1),
-            "d0": lambda q: subtract_h(q, 0), "d1": lambda q: subtract_h(q, 1),
             "x0": lambda q: gate(q, 0), "x1": lambda q: gate(q, 1),
             "n": noise_bias,
             "u0": lambda q: add_i(q, 0), "u1": lambda q: add_i(q, 1),
             "t0": lambda q: tanh_i(q, 0), "t1": lambda q: tanh_i(q, 1),
             "rn": relu_new, "rv": lambda q: relu_part(q, "V"), "rg": lambda q: relu_part(q, "G"), "rs": lambda q: relu_part(q, "S"), "sg": store_gate, "o0": lambda q: outputs(q, 0), "o1": lambda q: outputs(q, 1),
-            "dd": lambda q: [subtract_h(q, a) for a in pairs(q)],
-            "xn": lambda q: [gate(q, a) for a in pairs(q) if not h_on_vector(FIRST[q] // 2 + a)],
-            "xa": lambda q: [gate(q, a) for a in pairs(q) if h_on_vector(FIRST[q] // 2 + a)],
-            "tt": lambda q: tanh_whole(q),
+            "hx": lambda q: [turn_h(q, a) for a in pairs(q)], "hn": lambda q: [negate_h(q, a) for a in pairs(q)],
             "L": load_g, "N": load_n,
-            "WL": load_w, "W": weights, "Bb": lambda q: bias_b(), "Bc": lambda q: bias_bc(), "G": lambda q: bias_g(), "Gc": bias_gc, "Ng": lambda q: negate(),
+            "WL": load_w, "Wc": weights_group, "W": lambda q: weights(q // 2, q % 2), "SW": swap, "Bb": lambda q: bias_b(), "Bc": lambda q: bias_bc(), "G": lambda q: bias_g(), "Gc": bias_gc, "Ng": lambda q: negate(),
         }
 
         def do(calls):

@@ -23,7 +23,7 @@ VT = {}
 VTD = 0
 NBW = 4
 PAIRED = 10
-ALONE = (3, 7, 11, 15, 19, 23, 27)
+ALONE = (5, 9, 13, 17, 21, 25, 27)
 GTL = {}
 PLAIN = 4
 LOOKAHEAD = 6
@@ -92,15 +92,19 @@ def tile_gatel0rdcell_pa_t_kernel(tc, x_t, h_tminus1, gate_noise, Wg, bg, Wr, br
     ORDER = (
         ("L", 5),
         ("N", 4),
+        ("i0", -1),
+        ("i1", -1),
         ("g0", 2),
         ("g1", 2),
-        ("e0", 2),
-        ("e1", 2),
+        ("hx", 0),
         ("br0", -1),
         ("br1", -1),
+        ("e0", 2),
+        ("e1", 2),
         ("q", 1),
         ("o0", -2),
         ("o1", -2),
+        ("hn", 0),
         ("x0", -1),
         ("x1", -1),
         ("n", 1),
@@ -108,7 +112,6 @@ def tile_gatel0rdcell_pa_t_kernel(tc, x_t, h_tminus1, gate_noise, Wg, bg, Wr, br
         ("mrb", 0),
         ("m0", 0),
         ("m1", 0),
-        ("hx", 0),
         ("Ra", 0),
         ("Rb", 0),
         ("rn", -1),
@@ -116,7 +119,6 @@ def tile_gatel0rdcell_pa_t_kernel(tc, x_t, h_tminus1, gate_noise, Wg, bg, Wr, br
         ("sg", -1),
         ("u0", 0),
         ("u1", 0),
-        ("hn", 0),
         ("t0", 0),
         ("t1", 0),
     )
@@ -259,7 +261,7 @@ def tile_gatel0rdcell_pa_t_kernel(tc, x_t, h_tminus1, gate_noise, Wg, bg, Wr, br
         ident_b = const.tile([P, P], BF16)
         b_f32 = const.tile([P, P], F32)
         br_col = const.tile([P, 2], F32)
-        bg_b = const.tile([P, D], BF16)
+        bg_b = const.tile([P, D], F32)
 
         bias_of = {}
 
@@ -386,7 +388,7 @@ def tile_gatel0rdcell_pa_t_kernel(tc, x_t, h_tminus1, gate_noise, Wg, bg, Wr, br
 
         def turn_h(q, a):
             if h_on_vector(FIRST[q] // 2 + a):
-                hp = psum.tile([P, 2, 2, P], BF16, tag="ph", bufs=PH_BANKS)
+                hp = psum.tile([P, 2, 2, P], BF16, tag="pu", bufs=PU_BANKS)
                 for i in range(2):
                     for f in range(2):
                         nc.tensor.transpose(hp[:, i, f, :], h_rows(q, a, a + 1)[:, 0, i, f * P : (f + 1) * P], ident_b[:])
@@ -398,11 +400,17 @@ def tile_gatel0rdcell_pa_t_kernel(tc, x_t, h_tminus1, gate_noise, Wg, bg, Wr, br
                 nc.vector.tensor_scalar_mul(out=nh[:], in0=hp_of[q, a][:], scalar1=-1.0)
                 nh_of[q, a] = nh
 
-        def back_r(q, a):
-            alone = h_on_vector(FIRST[q] // 2 + a)
+        def minus_h(q, a):
             ph = psum.tile([P, 2, D], F32, tag="ph", bufs=PH_BANKS)
-            if not alone:
+            ph_of[(q, a)] = ph
+            if not h_on_vector(FIRST[q] // 2 + a):
                 nc.tensor.matmul(out=ph[:], lhsT=neg_ident[:], rhs=h_rows(q, a, a + 1)[:, 0], start=True, stop=False)
+
+        def back_r(q, a):
+            if (q, a) not in ph_of:
+                minus_h(q, a)
+            alone = h_on_vector(FIRST[q] // 2 + a)
+            ph = ph_of[(q, a)]
             for i in range(2):
                 c = (i * (UNITS[q] // 2) + a)
                 for f in range(2):
@@ -419,7 +427,6 @@ def tile_gatel0rdcell_pa_t_kernel(tc, x_t, h_tminus1, gate_noise, Wg, bg, Wr, br
                         nc.tensor.matmul(
                             out=region, lhsT=nh_of[q, a][:, i, f, :], rhs=ident[:], is_transpose=True, start=False, stop=True
                         )
-            ph_of[(q, a)] = ph
 
         def gate(q, a):
             pool = (nepool, e1pool)[a]
@@ -500,6 +507,7 @@ def tile_gatel0rdcell_pa_t_kernel(tc, x_t, h_tminus1, gate_noise, Wg, bg, Wr, br
             "mra": lambda q: mx_r(q, 0), "mrb": lambda q: mx_r(q, 1),
             "m0": lambda q: mx_gate(q, 0), "m1": lambda q: mx_gate(q, 1),
             "Ra": lambda q: tanh_r(q, 0), "Rb": lambda q: tanh_r(q, 1),
+            "i0": lambda q: minus_h(q, 0), "i1": lambda q: minus_h(q, 1),
             "br0": lambda q: back_r(q, 0), "br1": lambda q: back_r(q, 1),
             "x0": lambda q: gate(q, 0), "x1": lambda q: gate(q, 1),
             "n": noise_bias,

from contextlib import ExitStack

import concourse.mybir as mybir
from concourse.masks import make_identity

FLOPS = 2 * 8192 * 512 * 512

F32 = mybir.dt.float32
BF16 = mybir.dt.bfloat16
U32 = mybir.dt.uint32
U8 = mybir.dt.uint8
FP8X4 = mybir.dt.float8_e4m3fn_x4
ALU = mybir.AluOpType
ACT = mybir.ActivationFunctionType

P = 128
D = 256
NT = 64
NPAIRS = NT // 2
UNITS = (2, 2, 4, 4, 4, 4, 4, 4, 4, 4, 4, 4, 4, 4, 4, 4, 2, 2)
NU = 18
VT = {}
VTD = 0
NBW = 4
PAIRED = 10
ALONE = (5, 9, 13, 17, 21, 25, 27)
GTL = {}
PLAIN = 4
LOOKAHEAD = 6
GT_BANKS, PT_BANKS, PH_BANKS, PU_BANKS = 2, 2, 2, 2


def h_on_vector(pair):
    return pair in ALONE


def tile_gatel0rdcell_pa_t_kernel(tc, x_t, h_tminus1, gate_noise, Wg, bg, Wr, br, out_0, out_1):
    nc = tc.nc
    assert len(UNITS) == NU and sum(UNITS) == NT
    FIRST = [sum(UNITS[:u]) for u in range(NU)]
    xf = x_t.rearrange("(p t) k -> p (t k)", t=NT)
    hf = h_tminus1.rearrange("(p t) k -> p (t k)", t=NT)
    nv = gate_noise.rearrange("(p t) k -> p t k", t=NT)
    o0v = out_0.rearrange("(p t) k -> p t k", t=NT)
    o1v = out_1.rearrange("(p t) k -> p t k", t=NT)

    HEAD = (
        ("L", 0),
        ("WL", 1),
        ("L", 1),
        ("WL", 0),
        ("N", 0),
        ("L", 2),
        ("N", 1),
        ("L", 3),
        ("N", 2),
        ("L", 4),
        ("N", 3),
        ("L", 5),
        ("N", 4),
        ("Ng", 0),
        ("Bb", 0),
        ("g0", 0),
        ("e0", 0),
        ("g0", 1),
        ("e0", 1),
        ("Wc", 1),
        ("SW", 1),
        ("W", 3),
        ("q", 0),
        ("Bc", 0),
        ("mra", 0),
        ("mrb", 0),
        ("Ra", 0),
        ("Rb", 0),
        ("Wc", 0),
        ("SW", 0),
        ("W", 2),
        ("q", 1),
        ("G", 0),
        ("Gc", 0),
        ("m0", 0),
        ("n", 0),
        ("g0", 2),
        ("e0", 2),
        ("g1", 2),
        ("e1", 2),
        ("n", 1),
        ("u0", 0),
        ("t0", 0),
    )
    ORDER = (
        ("L", 5),
        ("N", 4),
        ("i0", -1),
        ("i1", -1),
        ("g0", 2),
        ("g1", 2),
        ("hx", 0),
        ("br0", -1),
        ("br1", -1),
        ("e0", 2),
        ("e1", 2),
        ("q", 1),
        ("o0", -2),
        ("o1", -2),
        ("hn", 0),
        ("x0", -1),
        ("x1", -1),
        ("n", 1),
        ("mra", 0),
        ("mrb", 0),
        ("m0", 0),
        ("m1", 0),
        ("Ra", 0),
        ("Rb", 0),
        ("rn", -1),
        ("rs", -1),
        ("sg", -1),
        ("u0", 0),
        ("u1", 0),
        ("t0", 0),
        ("t1", 0),
    )
    AFTER = {2: (
        ("W", 1),
        ("W", 0),
    )}
    with ExitStack() as ctx:
        const = ctx.enter_context(tc.tile_pool(name="const", bufs=1))
        npool = ctx.enter_context(tc.tile_pool(name="npool", bufs=4))
        grpool = ctx.enter_context(tc.tile_pool(name="grpool", bufs=3))
        cpool = ctx.enter_context(tc.tile_pool(name="cpool", bufs=5))
        hpool = ctx.enter_context(tc.tile_pool(name="hpool", bufs=4))
        upool = ctx.enter_context(tc.tile_pool(name="upool", bufs=3))
        tpool = ctx.enter_context(tc.tile_pool(name="tpool", bufs=3))
        dpool = ctx.enter_context(tc.tile_pool(name="dpool", bufs=3))
        nepool = ctx.enter_context(tc.tile_pool(name="nepool", bufs=3))
        e1pool = ctx.enter_context(tc.tile_pool(name="e1pool", bufs=3))
        opool = ctx.enter_context(tc.tile_pool(name="opool", bufs=3))
        psum = ctx.enter_context(tc.psum_pool(name="psum", bufs=2))

        nz_of = {}
        gt_of = {}
        gr_of = {}
        gc_of = {}
        gs_of = {}
        pt_of = {}
        hT_of = {}
        ph_of = {}
        pu_of = {}
        nb_of = {}
        u_of = {}
        t_of = {}
        e_of = {}
        lam_of = {}
        ht_of = {}
        lams = {}
        hts = {}
        hp_of = {}
        nh_of = {}

        def rows_of(q):
            return slice(FIRST[q], FIRST[q] + UNITS[q])

        gall = const.tile([P, NPAIRS * 4 * D], BF16)
        g_pairs = gall[:].rearrange("p (n c) -> p n c", c=4 * D)
        g_slots = gall[:].rearrange("p (n s d) -> p n s d", s=4, d=D)
        g_words = gall[:].bitcast(F32)

        def pairs_of(q):
            return FIRST[q] // 2, (FIRST[q] + UNITS[q]) // 2

        def load_g(q):
            a, b = pairs_of(q)
            if q < PLAIN:
                nc.sync.dma_start(out=g_slots[:, a:b, 0::2, :].rearrange("p n s d -> p (n s) d"), in_=xf[:, a * 2 * D : b * 2 * D].rearrange("p (t d) -> p t d", d=D))
                nc.sync.dma_start(out=g_slots[:, a:b, 1::2, :].rearrange("p n s d -> p (n s) d"), in_=hf[:, a * 2 * D : b * 2 * D].rearrange("p (t d) -> p t d", d=D))
                return
            if q == PLAIN:
                nc.sync.dma_start(out=gall[:, 4 * a * D : (4 * a + 1) * D], in_=hf[:, 2 * a * D : (2 * a + 1) * D])
            nc.sync.dma_start(
                out=g_pairs[:, a:b, D : 3 * D],
                in_=xf[:, a * 2 * D : b * 2 * D].rearrange("p (n c) -> p n c", c=2 * D),
            )
            last = b == NPAIRS
            if last:
                b = b - 1
            if b > a:
                nc.sync.dma_start(
                    out=gall[:, (4 * a + 3) * D : (4 * b + 3) * D].rearrange("p (n c) -> p n c", c=4 * D)[:, :, 0 : 2 * D],
                    in_=hf[:, (2 * a + 1) * D : (2 * b + 1) * D].rearrange("p (n c) -> p n c", c=2 * D),
                )
            if last:
                nc.sync.dma_start(out=gall[:, (4 * b + 3) * D : (4 * b + 4) * D], in_=hf[:, (2 * b + 1) * D : (2 * b + 2) * D])

        def h_rows(q, n0, n1):
            a, b = pairs_of(q)
            if q < PLAIN:
                return g_slots[:, a + n0 : a + n1, 1::2, :]
            return g_slots[:, a + n0 : a + n1, 0::3, :]

        def load_n(q):
            if q % 2:
                return
            lo, hi = FIRST[q], FIRST[q] + UNITS[q] + UNITS[q + 1]
            nz = npool.tile([P, hi - lo, D], BF16)
            nc.sync.dma_start(out=nz[:], in_=nv[:, lo:hi, :])
            nz_of[q] = nz[:, 0 : UNITS[q], :]
            nz_of[q + 1] = nz[:, UNITS[q] : hi - lo, :]

        b_rows = const.tile([P, P], BF16)
        nc.vector.memset(b_rows[:], 0.0)
        bg_row = const.tile([P, D], BF16)
        nc.vector.memset(bg_row[:], 0.0)
        warm = const.tile([P, 1], F32)
        nc.vector.memset(warm[:], 0.0)
        ones = const.tile([P, P], BF16)
        nc.vector.memset(ones[:], 1.0)
        nc.scalar.dma_start(out=b_rows[0:2, :], in_=br.rearrange("(f p) -> f p", p=P))
        nc.scalar.dma_start(out=bg_row[0:1, :], in_=bg.rearrange("(o n) -> o n", o=1))
        nc.scalar.activation(out=warm[:], in_=warm[:], func=ACT.Tanh)

        ident = const.tile([P, P], F32)
        make_identity(nc, ident[:])
        w_raw = const.tile([P, 2, 4, D], BF16)
        H = P // 2

        def load_w(m):
            nc.sync.dma_start(out=w_raw[:, m], in_=(Wg, Wr)[m].rearrange("(p j) w -> p j w", j=4))

        w_grp = const.tile([P, 2, 2, D, 4], BF16, align_bytes=64)
        w_codes = const.tile([P, 4 * D], U32, align_bytes=64)
        w_scales = const.tile([P, 4 * D], U8, align_bytes=64)

        def w_cols(side, m, lo, hi):
            return slice((2 * side + m) * D + lo, (2 * side + m) * D + hi)

        def weights_group(m):
            nc.vector.tensor_copy(out=w_grp[:, 1, m], in_=w_raw[:, m].rearrange("p j w -> p w j"))

        def swap(m):
            nc.sync.dma_start(out=w_grp[0:H, 0, m], in_=w_grp[H:P, 1, m])
            nc.sync.dma_start(out=w_grp[H:P, 0, m], in_=w_grp[0:H, 1, m])

        def copy_on(eng, out, in_):
            if eng:
                nc.scalar.copy(out=out, in_=in_)
            else:
                nc.vector.tensor_copy(out=out, in_=in_)

        def weights(side, m):
            cols = w_cols(side, m, 0, D)
            nc.vector.quantize_mx(
                out=w_codes[:, cols].bitcast(FP8X4),
                scales=w_scales[:, cols],
                in_=w_grp[:, side, m].rearrange("p w j -> p (w j)"),
            )

        neg_ident = const.tile([P, P], BF16)
        ident_b = const.tile([P, P], BF16)
        b_f32 = const.tile([P, P], F32)
        br_col = const.tile([P, 2], F32)
        bg_b = const.tile([P, D], F32)

        bias_of = {}

        def bias_b():
            nc.scalar.copy(out=b_f32[:], in_=b_rows[:])
            b_ps = psum.tile([P, 2, D], F32, tag="ph")
            nc.tensor.transpose(b_ps[:, 0, 0:P], b_f32[:], ident[:])
            bias_of["r"] = b_ps

        def bias_bc():
            nc.vector.tensor_copy(out=br_col[:], in_=bias_of["r"][:, 0, 0:2])

        def bias_g():
            bg_ps = psum.tile([P, 2, D], F32, tag="pu")
            nc.tensor.matmul(out=bg_ps[:, 0, :], lhsT=ones[:], rhs=bg_row[:], start=True, stop=True)
            bias_of["g"] = bg_ps

        def bias_gc(eng):
            if eng:
                nc.scalar.copy(out=bg_b[:], in_=bias_of["g"][:, 0, :])
            else:
                nc.vector.tensor_copy(out=bg_b[:], in_=bias_of["g"][:, 0, :])

        def negate():
            nc.scalar.mul(out=neg_ident[:], in_=ident[:], mul=-1.0)
            nc.scalar.copy(out=ident_b[:], in_=ident[:])

        def g_transposes(q, a):
            gt = psum.tile([P, 2, 2, P], F32, tag="gt", bufs=GT_BANKS)
            n = UNITS[q] // 2
            for i in range(2):
                pair, side = (2 * a + i) % n, (2 * a + i) // n
                w0 = (4 * (FIRST[q] // 2 + pair) + 2 * side) * (D // 2)
                for e in range(2):
                    nc.tensor.transpose(gt[:, e, i, :], g_words[:, w0 + e : w0 + D : 2], ident[:])
            gt_of[(q, a)] = gt

        def g_evacuate(q, a):
            if a == 0:
                gr_new = grpool.tile([P, UNITS[q] * 4 * P], BF16, align_bytes=64)
                gr_of[q] = gr_new
            nc.scalar.copy(
                out=gr_of[q][:, a * 8 * P : (a + 1) * 8 * P].bitcast(F32).rearrange("p (c e) -> p c e", e=2),
                in_=gt_of[(q, a)][:].rearrange("p e i l -> p (i l) e"),
            )

        def g_quantise(q):
            gc = cpool.tile([P, UNITS[q] * P], U32, align_bytes=64)
            gs = cpool.tile([P, UNITS[q] * P], U8, align_bytes=64)
            nc.vector.quantize_mx(out=gc[:].bitcast(FP8X4), scales=gs[:], in_=gr_of[q][:])
            gc_of[q] = gc
            gs_of[q] = gs

        def mx_r(q, f):
            pt = psum.tile([P, UNITS[q] * P], F32, tag="pt", bufs=PT_BANKS)
            half = UNITS[q] // 2 * P
            for side in range(2):
                if q < PLAIN and side == 1:
                    continue
                wcols = w_cols(1 if q < PLAIN else side, 1, f * P, (f + 1) * P)
                cols = slice(0, 2 * half) if q < PLAIN else slice(side * half, (side + 1) * half)
                nc.tensor.matmul_mx(
                    out=pt[:, cols],
                    lhsT=w_codes[:, wcols].bitcast(FP8X4),
                    lhsT_scale=w_scales[:, wcols],
                    rhs=gc_of[q][:, cols].bitcast(FP8X4),
                    rhs_scale=gs_of[q][:, cols],
                    start=True,
                    stop=True,
                )
            pt_of[(q, f)] = pt

        def mx_gate(q, a):
            pu = psum.tile([P, 2, D], F32, tag="pu", bufs=PU_BANKS)
            for i in range(2):
                c = i * (UNITS[q] // 2) + a
                cols = slice(c * P, (c + 1) * P)
                wcols = w_cols(1 if q < PLAIN else i, 0, 0, D)
                nc.tensor.matmul_mx(
                    out=pu[:, i, :],
                    lhsT=gc_of[q][:, cols].bitcast(FP8X4),
                    lhsT_scale=gs_of[q][:, cols],
                    rhs=w_codes[:, wcols].bitcast(FP8X4),
                    rhs_scale=w_scales[:, wcols],
                    start=True,
                    stop=True,
                )
            pu_of[(q, a)] = pu

        def tanh_r(q, f):
            hT = hpool.tile([P, UNITS[q] * P], F32)
            nc.scalar.activation(
                out=hT[:], in_=pt_of[(q, f)][:], func=ACT.Tanh, bias=br_col[:, f : f + 1], scale=1.0
            )
            hT_of[(q, f)] = hT

        def noise_bias(q):
            nb = nepool.tile([P, UNITS[q], D], F32, tag="ne")
            for i in range(0, UNITS[q], NBW):
                n = min(NBW, UNITS[q])
                nc.gpsimd.tensor_tensor(
                    out=nb[:, i : i + n, :],
                    in0=nz_of[q][:, i : i + n, :],
                    in1=bg_b[:].unsqueeze(1).to_broadcast([P, n, D]),
                    op=ALU.subtract,
                )
            nb_of[q] = nb

        def add_i(q, a):
            if a == 0:
                u_new = upool.tile([P, UNITS[q], D], F32)
                u_of[q] = u_new
            two = slice(2 * a, 2 * a + 2)
            nc.vector.tensor_tensor(
                out=u_of[q][:, two, :], in0=pu_of[(q, a)][:], in1=nb_of[q][:, two, :], op=ALU.subtract
            )

        def tanh_i(q, a):
            if a == 0:
                t_new = tpool.tile([P, UNITS[q], D], F32)
                t_of[q] = t_new
            two = slice(2 * a, 2 * a + 2)
            nc.scalar.activation(out=t_of[q][:, two, :], in_=u_of[q][:, two, :], func=ACT.Tanh)

        def turn_h(q, a):
            if h_on_vector(FIRST[q] // 2 + a):
                hp = psum.tile([P, 2, 2, P], BF16, tag="pu", bufs=PU_BANKS)
                for i in range(2):
                    for f in range(2):
                        nc.tensor.transpose(hp[:, i, f, :], h_rows(q, a, a + 1)[:, 0, i, f * P : (f + 1) * P], ident_b[:])
                hp_of[q, a] = hp

        def negate_h(q, a):
            if h_on_vector(FIRST[q] // 2 + a):
                nh = dpool.tile([P, 2, 2, P], F32)
                nc.vector.tensor_scalar_mul(out=nh[:], in0=hp_of[q, a][:], scalar1=-1.0)
                nh_of[q, a] = nh

        def minus_h(q, a):
            ph = psum.tile([P, 2, D], F32, tag="ph", bufs=PH_BANKS)
            ph_of[(q, a)] = ph
            if not h_on_vector(FIRST[q] // 2 + a):
                nc.tensor.matmul(out=ph[:], lhsT=neg_ident[:], rhs=h_rows(q, a, a + 1)[:, 0], start=True, stop=False)

        def back_r(q, a):
            if (q, a) not in ph_of:
                minus_h(q, a)
            alone = h_on_vector(FIRST[q] // 2 + a)
            ph = ph_of[(q, a)]
            for i in range(2):
                c = (i * (UNITS[q] // 2) + a)
                for f in range(2):
                    region = ph[:, i, f * P : (f + 1) * P]
                    nc.tensor.matmul(
                        out=region,
                        lhsT=hT_of[(q, f)][:, c * P : (c + 1) * P],
                        rhs=ident[:],
                        is_transpose=True,
                        start=alone,
                        stop=not alone and i == 1 and f == 1,
                    )
                    if alone:
                        nc.tensor.matmul(
                            out=region, lhsT=nh_of[q, a][:, i, f, :], rhs=ident[:], is_transpose=True, start=False, stop=True
                        )

        def gate(q, a):
            pool = (nepool, e1pool)[a]
            e_new = pool.tile([P, 2, D], F32, tag=("ne", "e1")[a])
            e_of[(q, a)] = e_new
            nc.vector.scalar_tensor_tensor(
                out=e_new[:],
                in0=t_of[q][:, 2 * a : 2 * a + 2, :],
                scalar=0.0,
                in1=ph_of[(q, a)][:],
                op0=ALU.max,
                op1=ALU.mult,
            )

        def store_group(q):
            if q < PAIRED:
                return q - q % 2, q - q % 2 + 1
            return q, q

        def out_tile(q, tiles, name):
            first, last = store_group(q)
            if q == first:
                new = opool.tile([P, FIRST[last] + UNITS[last] - FIRST[first], D], F32, name=name)
                tiles[first] = new
            lo = FIRST[q] - FIRST[first]
            tiles[q, 0] = tiles[first][:, lo : lo + UNITS[q], :]

        def store(q, tiles, view):
            first, last = store_group(q)
            if q == last:
                nc.sync.dma_start(out=view[:, FIRST[first] : FIRST[last] + UNITS[last], :], in_=tiles[first][:])

        def relu_new(q):
            out_tile(q, lams, "lam")
            lam_of[q] = lams[q, 0]

        def relu_part(q, eng):
            v, g = VT.get(q, VTD if UNITS[q] == 4 else 0), GTL.get(q, 0)
            if eng == "V" and v:
                nc.vector.tensor_scalar_max(out=lam_of[q][:, 0:v, :], in0=t_of[q][:, 0:v, :], scalar1=0.0)
            if eng == "G" and g:
                nc.gpsimd.tensor_scalar(out=lam_of[q][:, v:v + g, :], in0=t_of[q][:, v:v + g, :], scalar1=0.0, scalar2=1.0, op0=ALU.max, op1=ALU.mult)
            if eng == "S" and v + g < UNITS[q]:
                nc.scalar.activation(out=lam_of[q][:, v + g:, :], in_=t_of[q][:, v + g:, :], func=ACT.Relu)

        def store_gate(q):
            store(q, lams, o1v)

        def outputs(q, a):
            if a == 0:
                out_tile(q, hts, "ht")
                ht_of[q] = hts[q, 0]
            two = slice(2 * a, 2 * a + 2)
            nc.vector.tensor_tensor(
                out=ht_of[q][:, two, :], in0=e_of[(q, a)][:], in1=h_rows(q, a, a + 1)[:, 0], op=ALU.add
            )
            if 2 * a + 2 == UNITS[q]:
                store(q, hts, o0v)

        def on(q):
            return 0 <= q < NU

        def pairs(q):
            return range(UNITS[q] // 2)

        done = set()

        def skip(tok, q):
            if (tok, q) in done or not on(q):
                return True
            done.add((tok, q))
            return tok[-1] == "1" and tok[0] != "W" and UNITS[q] == 2

        STAGES = {
            "g0": lambda q: g_transposes(q, 0), "g1": lambda q: g_transposes(q, 1),
            "e0": lambda q: g_evacuate(q, 0), "e1": lambda q: g_evacuate(q, 1),
            "q": g_quantise,
            "mra": lambda q: mx_r(q, 0), "mrb": lambda q: mx_r(q, 1),
            "m0": lambda q: mx_gate(q, 0), "m1": lambda q: mx_gate(q, 1),
            "Ra": lambda q: tanh_r(q, 0), "Rb": lambda q: tanh_r(q, 1),
            "i0": lambda q: minus_h(q, 0), "i1": lambda q: minus_h(q, 1),
            "br0": lambda q: back_r(q, 0), "br1": lambda q: back_r(q, 1),
            "x0": lambda q: gate(q, 0), "x1": lambda q: gate(q, 1),
            "n": noise_bias,
            "u0": lambda q: add_i(q, 0), "u1": lambda q: add_i(q, 1),
            "t0": lambda q: tanh_i(q, 0), "t1": lambda q: tanh_i(q, 1),
            "rn": relu_new, "rv": lambda q: relu_part(q, "V"), "rg": lambda q: relu_part(q, "G"), "rs": lambda q: relu_part(q, "S"), "sg": store_gate, "o0": lambda q: outputs(q, 0), "o1": lambda q: outputs(q, 1),
            "hx": lambda q: [turn_h(q, a) for a in pairs(q)], "hn": lambda q: [negate_h(q, a) for a in pairs(q)],
            "L": load_g, "N": load_n,
            "WL": load_w, "Wc": weights_group, "W": lambda q: weights(q // 2, q % 2), "SW": swap, "Bb": lambda q: bias_b(), "Bc": lambda q: bias_bc(), "G": lambda q: bias_g(), "Gc": bias_gc, "Ng": lambda q: negate(),
        }

        def do(calls):
            for tok, q in calls:
                if not skip(tok, q):
                    STAGES[tok](q)

        def step(k, order):
            for tok, shift in order:
                if not skip(tok, k + shift):
                    STAGES[tok](k + shift)

        with tc.manual_schedule():
            do(HEAD)
            for k in range(0, NU + 3):
                step(k, ORDER)
                do(AFTER.get(k, ()))
